import numpy as np
import ml_dtypes

BF16 = ml_dtypes.bfloat16


def bf(x):
    return np.asarray(x, np.float32).astype(BF16)


def f32(x):
    return np.asarray(x, np.float32)


def f64(x):
    return np.asarray(x).astype(np.float64)


def striped(idx):
    return np.tile(idx.reshape(-1, 16).T, (8, 1))


DIM, S, H, M, ND, D, N = 128, 2048, 4, 512, 128, 8, 1024
SLOPE = 0.01


def setup_inputs():
    return {
        "table": bf(np.random.standard_normal((DIM, S))),
        "w": bf(np.random.standard_normal((DIM, M)) / np.sqrt(DIM)),
        "a1": f32(np.random.standard_normal((M, 1)) / np.sqrt(DIM)),
        "a2": f32(np.random.standard_normal((M, 1)) / np.sqrt(DIM)),
        "offs": striped(np.random.permutation(np.tile(np.arange(S), 2))[:N]),
    }


def reference(table, w, a1, a2, offs):
    idx = offs[:16].T.reshape(-1)
    t = f64(table)
    whj = f64(w).T @ t[:, idx]
    whd = f64(w).T @ t[:, :ND]
    nb = (f64(a2) * whj).reshape(H, DIM, ND, D).sum(axis=1)
    src = (f64(a1) * whd).reshape(H, DIM, ND).sum(axis=1)
    z = src[:, :, None] + nb
    e = np.maximum(z, SLOPE * z)
    p = np.exp(e - e.max(axis=2, keepdims=True))
    att = p / p.sum(axis=2, keepdims=True)
    agg = (att[:, None, :, :] * whj.reshape(H, DIM, ND, D)).sum(axis=3)
    return np.maximum(agg, 0.0).reshape(M, ND)

@@ -1,0 +1,164 @@
+import concourse.mybir as mybir
+
+F32 = mybir.dt.float32
+BF16 = mybir.dt.bfloat16
+U16 = mybir.dt.uint16
+ALU = mybir.AluOpType
+ACT = mybir.ActivationFunctionType
+X = mybir.AxisListType.X
+
+P = 128
+S = 2048
+H = 4
+D = 8
+N = P * D
+SLOPE = 0.01
+
+PIECE = 512
+BLOCK = 256
+N_BLOCKS = N // BLOCK
+BLOCK_NODES = BLOCK // D
+ROWS = N_BLOCKS * H
+PER_COL = 16
+
+FLOPS = 2 * P * (H * P) * (N + P)
+
+
+def tile_multihead_gaatn_kernel(tc, table, w, a1, a2, offs, out):
+    nc = tc.nc
+    with (
+        tc.tile_pool(name="held", bufs=1) as held,
+        tc.tile_pool(name="ring", bufs=3) as ring,
+        tc.psum_pool(name="bank_psum", bufs=1) as bank_psum,
+        tc.psum_pool(name="att_psum", bufs=4) as att_psum,
+    ):
+        w_sb = held.tile([P, H * P], BF16, name="w_sb")
+        nc.scalar.dma_start(w_sb[:], w)
+        a1_all = held.tile([P, H * P], F32, name="a1_all")
+        nc.sync.dma_start(a1_all[:], a1.rearrange("c o -> (c o)").partition_broadcast(P))
+        a2_all = held.tile([P, H * P], F32, name="a2_all")
+        nc.scalar.dma_start(a2_all[:], a2.rearrange("c o -> (c o)").partition_broadcast(P))
+        offsets = held.tile([P, N // PER_COL], U16, name="offsets")
+        nc.sync.dma_start(offsets[:], offs)
+        table_sb = held.tile([P, S], BF16, name="table_sb")
+        chunk = S // 4
+        for c in range(4):
+            queue = nc.sync if c % 2 == 0 else nc.scalar
+            queue.dma_start(table_sb[:, c * chunk : (c + 1) * chunk], table[:, c * chunk : (c + 1) * chunk])
+
+        warm = held.tile([P, 1], F32, name="warm")
+        nc.vector.memset(warm[:], 0.0)
+        nc.scalar.activation(warm[:], warm[:], ACT.Exp)
+        u_weights = held.tile([P, N_BLOCKS * (P + H)], BF16, name="u_weights")
+        nc.gpsimd.memset(u_weights[:], 0.0)
+        v_weights = held.tile([P, N_BLOCKS * (P + H)], BF16, name="v_weights")
+        nc.gpsimd.memset(v_weights[:], 0.0)
+        select = held.tile([P, ROWS, P], F32, name="select")
+        nc.gpsimd.memset(select[:], 0.0)
+        nc.gpsimd.affine_select(
+            out=select[:],
+            in_=select[:],
+            pattern=[[-1, ROWS], [0, P]],
+            compare_op=ALU.not_equal,
+            fill=1.0,
+            base=0,
+            channel_multiplier=1,
+        )
+
+        w_times_a1 = held.tile([P, H, P], F32, name="w_times_a1")
+        nc.vector.tensor_tensor(w_times_a1[:].rearrange("p k m -> p (k m)"), w_sb[:], a1_all[:], ALU.mult)
+        w_times_a2 = held.tile([P, H, P], F32, name="w_times_a2")
+        nc.vector.tensor_tensor(w_times_a2[:].rearrange("p k m -> p (k m)"), w_sb[:], a2_all[:], ALU.mult)
+        u = held.tile([P, H], F32, name="u")
+        nc.vector.tensor_reduce(u[:], w_times_a1[:], X, ALU.add)
+        v = held.tile([P, H], F32, name="v")
+        nc.vector.tensor_reduce(v[:], w_times_a2[:], X, ALU.add)
+        for vectors, weights in ((u, u_weights), (v, v_weights)):
+            nc.vector.tensor_copy(
+                weights[:].rearrange("p (b x) -> p b x", x=P + H)[:, :, 0:H],
+                vectors[:].unsqueeze(1).to_broadcast([P, N_BLOCKS, H]),
+            )
+
+        banks = [bank_psum.tile([P, PIECE], F32, name="bank" + str(i)) for i in range(2)]
+        src_ps = banks[0][:, 0:BLOCK_NODES]
+        for b in range(N_BLOCKS):
+            nc.tensor.matmul(
+                src_ps,
+                u_weights[:, b * P : (b + 1) * P],
+                table_sb[:, b * BLOCK_NODES : (b + 1) * BLOCK_NODES],
+                start=(b == 0),
+                stop=(b == N_BLOCKS - 1),
+            )
+        src = held.tile([P, BLOCK_NODES], F32, name="src")
+        nc.scalar.copy(src[:], src_ps)
+        nb_ps = banks[1][:, 0:BLOCK]
+        block_cols = BLOCK // PER_COL
+        for b in range(N_BLOCKS):
+            nc.tensor.matmul(
+                nb_ps,
+                v_weights[:, b * P : (b + 1) * P],
+                table_sb[:].indirect(offsets[:, b * block_cols : (b + 1) * block_cols]),
+                start=(b == 0),
+                stop=(b == N_BLOCKS - 1),
+            )
+
+        by_node = [P, BLOCK_NODES, D]
+        z = held.tile(by_node, F32, name="z")
+        nc.vector.tensor_tensor(
+            z[:], nb_ps.rearrange("p (n t) -> p n t", t=D), src[:].unsqueeze(2).to_broadcast(by_node), ALU.add
+        )
+        e = held.tile(by_node, F32, name="e")
+        nc.vector.scalar_tensor_tensor(e[:], z[:], SLOPE, z[:], ALU.mult, ALU.max)
+        e_max = held.tile([P, BLOCK_NODES], F32, name="e_max")
+        nc.vector.tensor_reduce(e_max[:], e[:], X, ALU.max)
+        shifted = held.tile(by_node, F32, name="shifted")
+        nc.vector.tensor_tensor(shifted[:], e[:], e_max[:].unsqueeze(2).to_broadcast(by_node), ALU.subtract)
+        p_exp = held.tile(by_node, F32, name="p_exp")
+        nc.scalar.activation(p_exp[:], shifted[:], ACT.Exp)
+        p_sum = held.tile([P, BLOCK_NODES], F32, name="p_sum")
+        nc.vector.tensor_reduce(p_sum[:], p_exp[:], X, ALU.add)
+        p_inv = held.tile([P, BLOCK_NODES], F32, name="p_inv")
+        nc.vector.reciprocal(p_inv[:], p_sum[:])
+        att = held.tile(by_node, F32, name="att")
+        nc.vector.tensor_tensor(att[:], p_exp[:], p_inv[:].unsqueeze(2).to_broadcast(by_node), ALU.mult)
+
+        whj = held.tile([P, H, N], F32, name="whj")
+        piece_cols = PIECE // PER_COL
+        for k in range(H):
+            for h in range(N // PIECE):
+                whj_ps = banks[(k * (N // PIECE) + h) % 2]
+                nc.tensor.matmul(
+                    whj_ps[:],
+                    w_sb[:, k * P : (k + 1) * P],
+                    table_sb[:].indirect(offsets[:, h * piece_cols : (h + 1) * piece_cols]),
+                    start=True,
+                    stop=True,
+                )
+                nc.scalar.copy(whj[:, k, h * PIECE : (h + 1) * PIECE], whj_ps[:])
+
+        piece_nodes = PIECE // D
+        for k in range(H):
+            agg = ring.tile([P, P], F32, name="agg")
+            for h in range(N // PIECE):
+                att_ps = att_psum.tile([P, PIECE], F32, name="att_ps")
+                for c in range(PIECE // BLOCK):
+                    b = h * (PIECE // BLOCK) + c
+                    nc.tensor.matmul(
+                        att_ps[:, c * BLOCK : (c + 1) * BLOCK],
+                        select[:, H * b + k, :],
+                        att[:].rearrange("p n t -> p (n t)"),
+                        start=True,
+                        stop=True,
+                    )
+                weighted = ring.tile([P, piece_nodes, D], F32, name="weighted")
+                nc.vector.tensor_tensor(
+                    weighted[:].rearrange("p n t -> p (n t)"),
+                    att_ps[:],
+                    whj[:, k, h * PIECE : (h + 1) * PIECE],
+                    ALU.mult,
+                )
+                nc.vector.tensor_reduce(agg[:, h * piece_nodes : (h + 1) * piece_nodes], weighted[:], X, ALU.add)
+            result = ring.tile([P, P], F32, name="result")
+            nc.scalar.activation(result[:], agg[:], ACT.Relu)
+            queue = nc.sync if k % 2 == 0 else nc.scalar
+            queue.dma_start(out[k * P : (k + 1) * P, :], result[:])

@@ -19,6 +19,8 @@ BLOCK = 256
 N_BLOCKS = N // BLOCK
 BLOCK_NODES = BLOCK // D
 ROWS = N_BLOCKS * H
+TERMS = 3
+GROUP = 32
 PER_COL = 16
 
 FLOPS = 2 * P * (H * P) * (N + P)
@@ -53,17 +55,27 @@ def tile_multihead_gaatn_kernel(tc, table, w, a1, a2, offs, out):
         nc.gpsimd.memset(u_weights[:], 0.0)
         v_weights = held.tile([P, N_BLOCKS * (P + H)], BF16, name="v_weights")
         nc.gpsimd.memset(v_weights[:], 0.0)
-        select = held.tile([P, ROWS, P], F32, name="select")
-        nc.gpsimd.memset(select[:], 0.0)
-        nc.gpsimd.affine_select(
-            out=select[:],
-            in_=select[:],
-            pattern=[[-1, ROWS], [0, P]],
-            compare_op=ALU.not_equal,
-            fill=1.0,
-            base=0,
-            channel_multiplier=1,
-        )
+        picks = held.tile([P, ROWS], F32, name="picks")
+        nc.gpsimd.memset(picks[:], 0.0)
+        for g in range(TERMS):
+            nc.gpsimd.affine_select(
+                out=picks[:],
+                in_=picks[:],
+                pattern=[[-1, ROWS]],
+                compare_op=ALU.not_equal,
+                fill=1.0,
+                base=-GROUP * g,
+                channel_multiplier=1,
+            )
+        select = held.tile([P, ROWS, P], BF16, name="select")
+        nc.gpsimd.tensor_copy(select[:], picks[:].unsqueeze(2).to_broadcast([P, ROWS, P]))
+        minus_hi = held.tile([P, 1], F32, name="minus_hi")
+        nc.vector.memset(minus_hi[0:GROUP, :], 0.0)
+        nc.vector.memset(minus_hi[GROUP : 2 * GROUP, :], -1.0)
+        nc.vector.memset(minus_hi[2 * GROUP : P, :], -1.0)
+        minus_mid = held.tile([P, 1], F32, name="minus_mid")
+        nc.vector.memset(minus_mid[0 : 2 * GROUP, :], 0.0)
+        nc.vector.memset(minus_mid[2 * GROUP : P, :], -1.0)
 
         w_times_a1 = held.tile([P, H, P], F32, name="w_times_a1")
         nc.vector.tensor_tensor(w_times_a1[:].rearrange("p k m -> p (k m)"), w_sb[:], a1_all[:], ALU.mult)
@@ -75,8 +87,10 @@ def tile_multihead_gaatn_kernel(tc, table, w, a1, a2, offs, out):
         nc.vector.tensor_reduce(v[:], w_times_a2[:], X, ALU.add)
         for vectors, weights in ((u, u_weights), (v, v_weights)):
             nc.vector.tensor_copy(
-                weights[:].rearrange("p (b x) -> p b x", x=P + H)[:, :, 0:H],
-                vectors[:].unsqueeze(1).to_broadcast([P, N_BLOCKS, H]),
+                weights[:]
+                .rearrange("p (b x) -> p b x", x=P + H)[:, :, 0 : TERMS * GROUP]
+                .rearrange("p b (g y) -> p b g y", y=GROUP)[:, :, :, 0:H],
+                vectors[:].unsqueeze(1).unsqueeze(1).to_broadcast([P, N_BLOCKS, TERMS, H]),
             )
 
         banks = [bank_psum.tile([P, PIECE], F32, name="bank" + str(i)) for i in range(2)]
@@ -121,6 +135,17 @@ def tile_multihead_gaatn_kernel(tc, table, w, a1, a2, offs, out):
         nc.vector.reciprocal(p_inv[:], p_sum[:])
         att = held.tile(by_node, F32, name="att")
         nc.vector.tensor_tensor(att[:], p_exp[:], p_inv[:].unsqueeze(2).to_broadcast(by_node), ALU.mult)
+        hi = held.tile(by_node, BF16, name="hi")
+        nc.vector.tensor_tensor(hi[:], p_exp[:], p_inv[:].unsqueeze(2).to_broadcast(by_node), ALU.mult)
+
+        att_flat = att[:].rearrange("p n t -> p (n t)")
+        hi_flat = hi[:].rearrange("p n t -> p (n t)")
+        rest = held.tile([P, BLOCK], F32, name="rest")
+        nc.vector.scalar_tensor_tensor(rest[:], hi_flat, minus_hi[:], att_flat, ALU.mult, ALU.add)
+        rest_bf = held.tile([P, BLOCK], BF16, name="rest_bf")
+        nc.vector.scalar_tensor_tensor(rest_bf[:], hi_flat, minus_hi[:], att_flat, ALU.mult, ALU.add)
+        term = held.tile([P, BLOCK], BF16, name="term")
+        nc.vector.scalar_tensor_tensor(term[:], rest_bf[:], minus_mid[:], rest[:], ALU.mult, ALU.add)
 
         whj = held.tile([P, H, N], F32, name="whj")
         piece_cols = PIECE // PER_COL
@@ -146,7 +171,7 @@ def tile_multihead_gaatn_kernel(tc, table, w, a1, a2, offs, out):
                     nc.tensor.matmul(
                         att_ps[:, c * BLOCK : (c + 1) * BLOCK],
                         select[:, H * b + k, :],
-                        att[:].rearrange("p n t -> p (n t)"),
+                        term[:],
                         start=True,
                         stop=True,
                     )

@@ -182,7 +182,9 @@ def tile_multihead_gaatn_kernel(tc, table, w, a1, a2, offs, out):
                     whj[:, k, h * PIECE : (h + 1) * PIECE],
                     ALU.mult,
                 )
-                nc.vector.tensor_reduce(agg[:, h * piece_nodes : (h + 1) * piece_nodes], weighted[:], X, ALU.add)
+                pairs = ring.tile([P, piece_nodes, D // 2], F32, name="pairs")
+                nc.gpsimd.tensor_tensor(pairs[:], weighted[:, :, 0 : D // 2], weighted[:, :, D // 2 : D], ALU.add)
+                nc.vector.tensor_reduce(agg[:, h * piece_nodes : (h + 1) * piece_nodes], pairs[:], X, ALU.add)
             result = ring.tile([P, P], F32, name="result")
             nc.scalar.activation(result[:], agg[:], ACT.Relu)
             queue = nc.sync if k % 2 == 0 else nc.scalar

@@ -15,13 +15,18 @@ N = P * D
 SLOPE = 0.01
 
 PIECE = 512
+N_PIECES = N // PIECE
 BLOCK = 256
 N_BLOCKS = N // BLOCK
 BLOCK_NODES = BLOCK // D
+HALVES = 2
+HALF_NODES = BLOCK_NODES // HALVES
+HALF = HALF_NODES * D
 ROWS = N_BLOCKS * H
 TERMS = 3
 GROUP = 32
 PER_COL = 16
+WARM_MATMULS = 12
 
 FLOPS = 2 * P * (H * P) * (N + P)
 
@@ -48,6 +53,11 @@ def tile_multihead_gaatn_kernel(tc, table, w, a1, a2, offs, out):
             queue = nc.sync if c % 2 == 0 else nc.scalar
             queue.dma_start(table_sb[:, c * chunk : (c + 1) * chunk], table[:, c * chunk : (c + 1) * chunk])
 
+        zeros = held.tile([P, PIECE], BF16, name="zeros")
+        nc.vector.memset(zeros[:], 0.0)
+        unused_ps = att_psum.tile([P, PIECE], F32, name="unused_ps", tag="att_ps")
+        for i in range(WARM_MATMULS):
+            nc.tensor.matmul(unused_ps[:], zeros[:, 0:P], zeros[:], start=True, stop=True)
         warm = held.tile([P, 1], F32, name="warm")
         nc.vector.memset(warm[:], 0.0)
         nc.scalar.activation(warm[:], warm[:], ACT.Exp)
@@ -93,19 +103,23 @@ def tile_multihead_gaatn_kernel(tc, table, w, a1, a2, offs, out):
                 vectors[:].unsqueeze(1).unsqueeze(1).to_broadcast([P, N_BLOCKS, TERMS, H]),
             )
 
-        banks = [bank_psum.tile([P, PIECE], F32, name="bank" + str(i)) for i in range(2)]
-        src_ps = banks[0][:, 0:BLOCK_NODES]
-        for b in range(N_BLOCKS):
-            nc.tensor.matmul(
-                src_ps,
-                u_weights[:, b * P : (b + 1) * P],
-                table_sb[:, b * BLOCK_NODES : (b + 1) * BLOCK_NODES],
-                start=(b == 0),
-                stop=(b == N_BLOCKS - 1),
-            )
-        src = held.tile([P, BLOCK_NODES], F32, name="src")
-        nc.scalar.copy(src[:], src_ps)
-        nb_ps = banks[1][:, 0:BLOCK]
+        banks = [bank_psum.tile([P, PIECE], F32, name="bank" + str(i)) for i in range(3)]
+        src = []
+        for half in range(HALVES):
+            src_ps = banks[half][:, 0:HALF_NODES]
+            for b in range(N_BLOCKS):
+                first_node = b * BLOCK_NODES + half * HALF_NODES
+                nc.tensor.matmul(
+                    src_ps,
+                    u_weights[:, b * P : (b + 1) * P],
+                    table_sb[:, first_node : first_node + HALF_NODES],
+                    start=(b == 0),
+                    stop=(b == N_BLOCKS - 1),
+                )
+            src_half = held.tile([P, HALF_NODES], F32, name="src" + str(half))
+            nc.scalar.copy(src_half[:], src_ps)
+            src.append(src_half)
+        nb_ps = banks[2][:, 0:BLOCK]
         block_cols = BLOCK // PER_COL
         for b in range(N_BLOCKS):
             nc.tensor.matmul(
@@ -116,42 +130,49 @@ def tile_multihead_gaatn_kernel(tc, table, w, a1, a2, offs, out):
                 stop=(b == N_BLOCKS - 1),
             )
 
-        by_node = [P, BLOCK_NODES, D]
-        z = held.tile(by_node, F32, name="z")
-        nc.vector.tensor_tensor(
-            z[:], nb_ps.rearrange("p (n t) -> p n t", t=D), src[:].unsqueeze(2).to_broadcast(by_node), ALU.add
-        )
-        e = held.tile(by_node, F32, name="e")
-        nc.vector.scalar_tensor_tensor(e[:], z[:], SLOPE, z[:], ALU.mult, ALU.max)
-        e_max = held.tile([P, BLOCK_NODES], F32, name="e_max")
-        nc.vector.tensor_reduce(e_max[:], e[:], X, ALU.max)
-        shifted = held.tile(by_node, F32, name="shifted")
-        nc.vector.tensor_tensor(shifted[:], e[:], e_max[:].unsqueeze(2).to_broadcast(by_node), ALU.subtract)
-        p_exp = held.tile(by_node, F32, name="p_exp")
-        nc.scalar.activation(p_exp[:], shifted[:], ACT.Exp)
-        p_sum = held.tile([P, BLOCK_NODES], F32, name="p_sum")
-        nc.vector.tensor_reduce(p_sum[:], p_exp[:], X, ALU.add)
-        p_inv = held.tile([P, BLOCK_NODES], F32, name="p_inv")
-        nc.vector.reciprocal(p_inv[:], p_sum[:])
-        att = held.tile(by_node, F32, name="att")
-        nc.vector.tensor_tensor(att[:], p_exp[:], p_inv[:].unsqueeze(2).to_broadcast(by_node), ALU.mult)
-        hi = held.tile(by_node, BF16, name="hi")
-        nc.vector.tensor_tensor(hi[:], p_exp[:], p_inv[:].unsqueeze(2).to_broadcast(by_node), ALU.mult)
+        by_node = [P, HALF_NODES, D]
+        terms = []
+        for half in range(HALVES):
+            of_half = str(half)
+            z = held.tile(by_node, F32, name="z" + of_half)
+            nc.vector.tensor_tensor(
+                z[:],
+                nb_ps[:, half * HALF : (half + 1) * HALF].rearrange("p (n t) -> p n t", t=D),
+                src[half][:].unsqueeze(2).to_broadcast(by_node),
+                ALU.add,
+            )
+            e = held.tile(by_node, F32, name="e" + of_half)
+            nc.vector.scalar_tensor_tensor(e[:], z[:], SLOPE, z[:], ALU.mult, ALU.max)
+            e_max = held.tile([P, HALF_NODES], F32, name="e_max" + of_half)
+            nc.vector.tensor_reduce(e_max[:], e[:], X, ALU.max)
+            shifted = held.tile(by_node, F32, name="shifted" + of_half)
+            nc.vector.tensor_tensor(shifted[:], e[:], e_max[:].unsqueeze(2).to_broadcast(by_node), ALU.subtract)
+            p_exp = held.tile(by_node, F32, name="p_exp" + of_half)
+            nc.scalar.activation(p_exp[:], shifted[:], ACT.Exp)
+            p_sum = held.tile([P, HALF_NODES], F32, name="p_sum" + of_half)
+            nc.vector.tensor_reduce(p_sum[:], p_exp[:], X, ALU.add)
+            p_inv = held.tile([P, HALF_NODES], F32, name="p_inv" + of_half)
+            nc.vector.reciprocal(p_inv[:], p_sum[:])
+            att = held.tile(by_node, F32, name="att" + of_half)
+            nc.vector.tensor_tensor(att[:], p_exp[:], p_inv[:].unsqueeze(2).to_broadcast(by_node), ALU.mult)
+            hi = held.tile(by_node, BF16, name="hi" + of_half)
+            nc.vector.tensor_tensor(hi[:], p_exp[:], p_inv[:].unsqueeze(2).to_broadcast(by_node), ALU.mult)
 
-        att_flat = att[:].rearrange("p n t -> p (n t)")
-        hi_flat = hi[:].rearrange("p n t -> p (n t)")
-        rest = held.tile([P, BLOCK], F32, name="rest")
-        nc.vector.scalar_tensor_tensor(rest[:], hi_flat, minus_hi[:], att_flat, ALU.mult, ALU.add)
-        rest_bf = held.tile([P, BLOCK], BF16, name="rest_bf")
-        nc.vector.scalar_tensor_tensor(rest_bf[:], hi_flat, minus_hi[:], att_flat, ALU.mult, ALU.add)
-        term = held.tile([P, BLOCK], BF16, name="term")
-        nc.vector.scalar_tensor_tensor(term[:], rest_bf[:], minus_mid[:], rest[:], ALU.mult, ALU.add)
+            att_flat = att[:].rearrange("p n t -> p (n t)")
+            hi_flat = hi[:].rearrange("p n t -> p (n t)")
+            rest = held.tile([P, HALF], F32, name="rest" + of_half)
+            nc.vector.scalar_tensor_tensor(rest[:], hi_flat, minus_hi[:], att_flat, ALU.mult, ALU.add)
+            rest_bf = held.tile([P, HALF], BF16, name="rest_bf" + of_half)
+            nc.vector.scalar_tensor_tensor(rest_bf[:], hi_flat, minus_hi[:], att_flat, ALU.mult, ALU.add)
+            term = held.tile([P, HALF], BF16, name="term" + of_half)
+            nc.vector.scalar_tensor_tensor(term[:], rest_bf[:], minus_mid[:], rest[:], ALU.mult, ALU.add)
+            terms.append(term)
 
         whj = held.tile([P, H, N], F32, name="whj")
         piece_cols = PIECE // PER_COL
         for k in range(H):
-            for h in range(N // PIECE):
-                whj_ps = banks[(k * (N // PIECE) + h) % 2]
+            for h in range(N_PIECES):
+                whj_ps = banks[(k * N_PIECES + h) % 3]
                 nc.tensor.matmul(
                     whj_ps[:],
                     w_sb[:, k * P : (k + 1) * P],
@@ -161,31 +182,24 @@ def tile_multihead_gaatn_kernel(tc, table, w, a1, a2, offs, out):
                 )
                 nc.scalar.copy(whj[:, k, h * PIECE : (h + 1) * PIECE], whj_ps[:])
 
-        piece_nodes = PIECE // D
-        for k in range(H):
-            agg = ring.tile([P, P], F32, name="agg")
-            for h in range(N // PIECE):
-                att_ps = att_psum.tile([P, PIECE], F32, name="att_ps")
-                for c in range(PIECE // BLOCK):
-                    b = h * (PIECE // BLOCK) + c
-                    nc.tensor.matmul(
-                        att_ps[:, c * BLOCK : (c + 1) * BLOCK],
-                        select[:, H * b + k, :],
-                        term[:],
-                        start=True,
-                        stop=True,
-                    )
-                weighted = ring.tile([P, piece_nodes, D], F32, name="weighted")
+        agg = held.tile([P, H, N_BLOCKS, BLOCK_NODES], F32, name="agg")
+        for half in range(HALVES):
+            for k in range(H):
+                att_ps = att_psum.tile([P, N_BLOCKS, HALF], F32, name="att_ps")
+                for b in range(N_BLOCKS):
+                    nc.tensor.matmul(att_ps[:, b, :], select[:, H * b + k, :], terms[half][:], start=True, stop=True)
+                weighted = ring.tile([P, N_BLOCKS, HALF_NODES, D], F32, name="weighted")
                 nc.vector.tensor_tensor(
-                    weighted[:].rearrange("p n t -> p (n t)"),
+                    weighted[:].rearrange("p b n t -> p b (n t)"),
                     att_ps[:],
-                    whj[:, k, h * PIECE : (h + 1) * PIECE],
+                    whj[:, k, :].rearrange("p (b c) -> p b c", c=BLOCK)[:, :, half * HALF : (half + 1) * HALF],
                     ALU.mult,
                 )
-                pairs = ring.tile([P, piece_nodes, D // 2], F32, name="pairs")
-                nc.gpsimd.tensor_tensor(pairs[:], weighted[:, :, 0 : D // 2], weighted[:, :, D // 2 : D], ALU.add)
-                nc.vector.tensor_reduce(agg[:, h * piece_nodes : (h + 1) * piece_nodes], pairs[:], X, ALU.add)
-            result = ring.tile([P, P], F32, name="result")
-            nc.scalar.activation(result[:], agg[:], ACT.Relu)
-            queue = nc.sync if k % 2 == 0 else nc.scalar
-            queue.dma_start(out[k * P : (k + 1) * P, :], result[:])
+                nc.vector.tensor_reduce(
+                    agg[:, k, :, half * HALF_NODES : (half + 1) * HALF_NODES], weighted[:], X, ALU.add
+                )
+                if half == HALVES - 1:
+                    result = ring.tile([P, P], F32, name="result")
+                    nc.scalar.activation(result[:], agg[:, k, :, :].rearrange("p b n -> p (b n)"), ACT.Relu)
+                    queue = nc.sync if k % 2 == 0 else nc.scalar
+                    queue.dma_start(out[k * P : (k + 1) * P, :], result[:])

@@ -26,7 +26,7 @@ ROWS = N_BLOCKS * H
 TERMS = 3
 GROUP = 32
 PER_COL = 16
-WARM_MATMULS = 12
+WARM_MATMULS = 6
 
 FLOPS = 2 * P * (H * P) * (N + P)
 
@@ -87,15 +87,15 @@ def tile_multihead_gaatn_kernel(tc, table, w, a1, a2, offs, out):
         nc.vector.memset(minus_mid[0 : 2 * GROUP, :], 0.0)
         nc.vector.memset(minus_mid[2 * GROUP : P, :], -1.0)
 
-        w_times_a1 = held.tile([P, H, P], F32, name="w_times_a1")
-        nc.vector.tensor_tensor(w_times_a1[:].rearrange("p k m -> p (k m)"), w_sb[:], a1_all[:], ALU.mult)
-        w_times_a2 = held.tile([P, H, P], F32, name="w_times_a2")
-        nc.vector.tensor_tensor(w_times_a2[:].rearrange("p k m -> p (k m)"), w_sb[:], a2_all[:], ALU.mult)
         u = held.tile([P, H], F32, name="u")
-        nc.vector.tensor_reduce(u[:], w_times_a1[:], X, ALU.add)
         v = held.tile([P, H], F32, name="v")
-        nc.vector.tensor_reduce(v[:], w_times_a2[:], X, ALU.add)
-        for vectors, weights in ((u, u_weights), (v, v_weights)):
+        for a_all, vectors, weights in ((a1_all, u, u_weights), (a2_all, v, v_weights)):
+            for k in range(H):
+                head = slice(k * P, (k + 1) * P)
+                products = ring.tile([P, P], F32, name="products")
+                nc.vector.scalar_tensor_tensor(
+                    products[:], w_sb[:, head], 1.0, a_all[:, head], ALU.mult, ALU.mult, accum_out=vectors[:, k : k + 1]
+                )
             nc.vector.tensor_copy(
                 weights[:]
                 .rearrange("p (b x) -> p b x", x=P + H)[:, :, 0 : TERMS * GROUP]

@@ -26,7 +26,6 @@ ROWS = N_BLOCKS * H
 TERMS = 3
 GROUP = 32
 PER_COL = 16
-WARM_MATMULS = 6
 
 FLOPS = 2 * P * (H * P) * (N + P)
 
@@ -53,11 +52,6 @@ def tile_multihead_gaatn_kernel(tc, table, w, a1, a2, offs, out):
             queue = nc.sync if c % 2 == 0 else nc.scalar
             queue.dma_start(table_sb[:, c * chunk : (c + 1) * chunk], table[:, c * chunk : (c + 1) * chunk])
 
-        zeros = held.tile([P, PIECE], BF16, name="zeros")
-        nc.vector.memset(zeros[:], 0.0)
-        unused_ps = att_psum.tile([P, PIECE], F32, name="unused_ps", tag="att_ps")
-        for i in range(WARM_MATMULS):
-            nc.tensor.matmul(unused_ps[:], zeros[:, 0:P], zeros[:], start=True, stop=True)
         warm = held.tile([P, 1], F32, name="warm")
         nc.vector.memset(warm[:], 0.0)
         nc.scalar.activation(warm[:], warm[:], ACT.Exp)

@@ -26,6 +26,7 @@ ROWS = N_BLOCKS * H
 TERMS = 3
 GROUP = 32
 PER_COL = 16
+WARM_MATMULS = 12
 
 FLOPS = 2 * P * (H * P) * (N + P)
 
@@ -52,6 +53,11 @@ def tile_multihead_gaatn_kernel(tc, table, w, a1, a2, offs, out):
             queue = nc.sync if c % 2 == 0 else nc.scalar
             queue.dma_start(table_sb[:, c * chunk : (c + 1) * chunk], table[:, c * chunk : (c + 1) * chunk])
 
+        zeros = held.tile([P, PIECE], BF16, name="zeros")
+        nc.vector.memset(zeros[:], 0.0)
+        unused_ps = att_psum.tile([P, PIECE], F32, name="unused_ps", tag="att_ps")
+        for i in range(WARM_MATMULS):
+            nc.tensor.matmul(unused_ps[:], zeros[:, 0:P], zeros[:], start=True, stop=True)
         warm = held.tile([P, 1], F32, name="warm")
         nc.vector.memset(warm[:], 0.0)
         nc.scalar.activation(warm[:], warm[:], ACT.Exp)

@@ -27,6 +27,7 @@ TERMS = 3
 GROUP = 32
 PER_COL = 16
 WARM_MATMULS = 12
+GPSIMD_HEADS = 2
 
 FLOPS = 2 * P * (H * P) * (N + P)
 
@@ -183,23 +184,41 @@ def tile_multihead_gaatn_kernel(tc, table, w, a1, a2, offs, out):
                 nc.scalar.copy(whj[:, k, h * PIECE : (h + 1) * PIECE], whj_ps[:])
 
         agg = held.tile([P, H, N_BLOCKS, BLOCK_NODES], F32, name="agg")
+
+        def spread_att(half, k):
+            att_ps = att_psum.tile([P, N_BLOCKS, HALF], F32, name="att_ps")
+            for b in range(N_BLOCKS):
+                nc.tensor.matmul(att_ps[:, b, :], select[:, H * b + k, :], terms[half][:], start=True, stop=True)
+            return att_ps
+
+        def whj_of(half, k):
+            return whj[:, k, :].rearrange("p (b c) -> p b c", c=BLOCK)[:, :, half * HALF : (half + 1) * HALF]
+
+        def sum_neighbours(half, k, weighted):
+            nc.vector.tensor_reduce(agg[:, k, :, half * HALF_NODES : (half + 1) * HALF_NODES], weighted[:], X, ALU.add)
+            if half == HALVES - 1:
+                result = held.tile([P, P], F32, name="result" + str(k))
+                nc.scalar.activation(result[:], agg[:, k, :, :].rearrange("p b n -> p (b n)"), ACT.Relu)
+                queue = nc.sync if k % 2 == 0 else nc.scalar
+                queue.dma_start(out[k * P : (k + 1) * P, :], result[:])
+
         for half in range(HALVES):
-            for k in range(H):
-                att_ps = att_psum.tile([P, N_BLOCKS, HALF], F32, name="att_ps")
-                for b in range(N_BLOCKS):
-                    nc.tensor.matmul(att_ps[:, b, :], select[:, H * b + k, :], terms[half][:], start=True, stop=True)
+            by_gpsimd = []
+            for k in range(H - GPSIMD_HEADS, H):
+                att_ps = spread_att(half, k)
+                att_sb = ring.tile([P, N_BLOCKS, HALF], F32, name="att_sb")
+                nc.scalar.copy(att_sb[:], att_ps[:])
+                weighted = ring.tile([P, N_BLOCKS, HALF_NODES, D], F32, name="weighted_g")
+                nc.gpsimd.tensor_tensor(
+                    weighted[:].rearrange("p b n t -> p b (n t)"), att_sb[:], whj_of(half, k), ALU.mult
+                )
+                by_gpsimd.append((k, weighted))
+            for k in range(H - GPSIMD_HEADS):
+                att_ps = spread_att(half, k)
                 weighted = ring.tile([P, N_BLOCKS, HALF_NODES, D], F32, name="weighted")
                 nc.vector.tensor_tensor(
-                    weighted[:].rearrange("p b n t -> p b (n t)"),
-                    att_ps[:],
-                    whj[:, k, :].rearrange("p (b c) -> p b c", c=BLOCK)[:, :, half * HALF : (half + 1) * HALF],
-                    ALU.mult,
+                    weighted[:].rearrange("p b n t -> p b (n t)"), att_ps[:], whj_of(half, k), ALU.mult
                 )
-                nc.vector.tensor_reduce(
-                    agg[:, k, :, half * HALF_NODES : (half + 1) * HALF_NODES], weighted[:], X, ALU.add
-                )
-                if half == HALVES - 1:
-                    result = ring.tile([P, P], F32, name="result")
-                    nc.scalar.activation(result[:], agg[:, k, :, :].rearrange("p b n -> p (b n)"), ACT.Relu)
-                    queue = nc.sync if k % 2 == 0 else nc.scalar
-                    queue.dma_start(out[k * P : (k + 1) * P, :], result[:])
+                sum_neighbours(half, k, weighted)
+            for k, weighted in by_gpsimd:
+                sum_neighbours(half, k, weighted)

@@ -79,7 +79,7 @@ def tile_multihead_gaatn_kernel(tc, table, w, a1, a2, offs, out):
                 channel_multiplier=1,
             )
         select = held.tile([P, ROWS, P], BF16, name="select")
-        nc.gpsimd.tensor_copy(select[:], picks[:].unsqueeze(2).to_broadcast([P, ROWS, P]))
+        nc.gpsimd.tensor_scalar(select[:], picks[:].unsqueeze(2).to_broadcast([P, ROWS, P]), 1.0, 0.0, ALU.mult, ALU.add)
         minus_hi = held.tile([P, 1], F32, name="minus_hi")
         nc.vector.memset(minus_hi[0:GROUP, :], 0.0)
         nc.vector.memset(minus_hi[GROUP : 2 * GROUP, :], -1.0)
@@ -202,17 +202,17 @@ def tile_multihead_gaatn_kernel(tc, table, w, a1, a2, offs, out):
                 queue = nc.sync if k % 2 == 0 else nc.scalar
                 queue.dma_start(out[k * P : (k + 1) * P, :], result[:])
 
+        def multiply_on_gpsimd(half, k):
+            att_ps = spread_att(half, k)
+            att_sb = ring.tile([P, N_BLOCKS, HALF], F32, name="att_sb")
+            nc.scalar.copy(att_sb[:], att_ps[:])
+            weighted = held.tile([P, N_BLOCKS, HALF_NODES, D], F32, name="weighted_g" + str(half) + str(k))
+            nc.gpsimd.tensor_tensor(weighted[:].rearrange("p b n t -> p b (n t)"), att_sb[:], whj_of(half, k), ALU.mult)
+            return half, k, weighted
+
+        unsummed = []
         for half in range(HALVES):
-            by_gpsimd = []
-            for k in range(H - GPSIMD_HEADS, H):
-                att_ps = spread_att(half, k)
-                att_sb = ring.tile([P, N_BLOCKS, HALF], F32, name="att_sb")
-                nc.scalar.copy(att_sb[:], att_ps[:])
-                weighted = ring.tile([P, N_BLOCKS, HALF_NODES, D], F32, name="weighted_g")
-                nc.gpsimd.tensor_tensor(
-                    weighted[:].rearrange("p b n t -> p b (n t)"), att_sb[:], whj_of(half, k), ALU.mult
-                )
-                by_gpsimd.append((k, weighted))
+            started = [multiply_on_gpsimd(half, k) for k in range(H - GPSIMD_HEADS, H)]
             for k in range(H - GPSIMD_HEADS):
                 att_ps = spread_att(half, k)
                 weighted = ring.tile([P, N_BLOCKS, HALF_NODES, D], F32, name="weighted")
@@ -220,5 +220,8 @@ def tile_multihead_gaatn_kernel(tc, table, w, a1, a2, offs, out):
                     weighted[:].rearrange("p b n t -> p b (n t)"), att_ps[:], whj_of(half, k), ALU.mult
                 )
                 sum_neighbours(half, k, weighted)
-            for k, weighted in by_gpsimd:
-                sum_neighbours(half, k, weighted)
+            for earlier_half, k, weighted in unsummed:
+                sum_neighbours(earlier_half, k, weighted)
+            unsummed = started
+        for last_half, k, weighted in unsummed:
+            sum_neighbours(last_half, k, weighted)

@@ -25,8 +25,8 @@ HALF = HALF_NODES * D
 ROWS = N_BLOCKS * H
 TERMS = 3
 GROUP = 32
+SHIFT = H * (N_BLOCKS - 1)
 PER_COL = 16
-WARM_MATMULS = 12
 GPSIMD_HEADS = 2
 
 FLOPS = 2 * P * (H * P) * (N + P)
@@ -54,18 +54,17 @@ def tile_multihead_gaatn_kernel(tc, table, w, a1, a2, offs, out):
             queue = nc.sync if c % 2 == 0 else nc.scalar
             queue.dma_start(table_sb[:, c * chunk : (c + 1) * chunk], table[:, c * chunk : (c + 1) * chunk])
 
-        zeros = held.tile([P, PIECE], BF16, name="zeros")
-        nc.vector.memset(zeros[:], 0.0)
-        unused_ps = att_psum.tile([P, PIECE], F32, name="unused_ps", tag="att_ps")
-        for i in range(WARM_MATMULS):
-            nc.tensor.matmul(unused_ps[:], zeros[:, 0:P], zeros[:], start=True, stop=True)
         warm = held.tile([P, 1], F32, name="warm")
         nc.vector.memset(warm[:], 0.0)
         nc.scalar.activation(warm[:], warm[:], ACT.Exp)
-        u_weights = held.tile([P, N_BLOCKS * (P + H)], BF16, name="u_weights")
+        u_weights = held.tile([P, SHIFT + P], BF16, name="u_weights")
         nc.gpsimd.memset(u_weights[:], 0.0)
-        v_weights = held.tile([P, N_BLOCKS * (P + H)], BF16, name="v_weights")
+        v_weights = held.tile([P, SHIFT + P], BF16, name="v_weights")
         nc.gpsimd.memset(v_weights[:], 0.0)
+
+        def weights_of_block(weights, b):
+            return weights[:, SHIFT - H * b : SHIFT - H * b + P]
+
         picks = held.tile([P, ROWS], F32, name="picks")
         nc.gpsimd.memset(picks[:], 0.0)
         for g in range(TERMS):
@@ -98,36 +97,27 @@ def tile_multihead_gaatn_kernel(tc, table, w, a1, a2, offs, out):
                     products[:], w_sb[:, head], 1.0, a_all[:, head], ALU.mult, ALU.mult, accum_out=vectors[:, k : k + 1]
                 )
             nc.vector.tensor_copy(
-                weights[:]
-                .rearrange("p (b x) -> p b x", x=P + H)[:, :, 0 : TERMS * GROUP]
-                .rearrange("p b (g y) -> p b g y", y=GROUP)[:, :, :, 0:H],
-                vectors[:].unsqueeze(1).unsqueeze(1).to_broadcast([P, N_BLOCKS, TERMS, H]),
+                weights[:, SHIFT : SHIFT + TERMS * GROUP].rearrange("p (g y) -> p g y", y=GROUP)[:, :, 0:H],
+                vectors[:].unsqueeze(1).to_broadcast([P, TERMS, H]),
             )
 
         banks = [bank_psum.tile([P, PIECE], F32, name="bank" + str(i)) for i in range(3)]
-        src = []
-        for half in range(HALVES):
-            src_ps = banks[half][:, 0:HALF_NODES]
-            for b in range(N_BLOCKS):
-                first_node = b * BLOCK_NODES + half * HALF_NODES
-                nc.tensor.matmul(
-                    src_ps,
-                    u_weights[:, b * P : (b + 1) * P],
-                    table_sb[:, first_node : first_node + HALF_NODES],
-                    start=(b == 0),
-                    stop=(b == N_BLOCKS - 1),
-                )
-            src_half = held.tile([P, HALF_NODES], F32, name="src" + str(half))
-            nc.scalar.copy(src_half[:], src_ps)
-            src.append(src_half)
-        nb_ps = banks[2][:, 0:BLOCK]
+        z_ps = banks[2][:, 0:BLOCK]
+        for b in range(N_BLOCKS):
+            nc.tensor.matmul(
+                z_ps.rearrange("p (n t) -> p n t", t=D),
+                weights_of_block(u_weights, b),
+                table_sb[:, b * BLOCK_NODES : (b + 1) * BLOCK_NODES].unsqueeze(2).to_broadcast([P, BLOCK_NODES, D]),
+                start=(b == 0),
+                stop=False,
+            )
         block_cols = BLOCK // PER_COL
         for b in range(N_BLOCKS):
             nc.tensor.matmul(
-                nb_ps,
-                v_weights[:, b * P : (b + 1) * P],
+                z_ps,
+                weights_of_block(v_weights, b),
                 table_sb[:].indirect(offsets[:, b * block_cols : (b + 1) * block_cols]),
-                start=(b == 0),
+                start=False,
                 stop=(b == N_BLOCKS - 1),
             )
 
@@ -135,17 +125,15 @@ def tile_multihead_gaatn_kernel(tc, table, w, a1, a2, offs, out):
         terms = []
         for half in range(HALVES):
             of_half = str(half)
-            z = held.tile(by_node, F32, name="z" + of_half)
-            nc.vector.tensor_tensor(
-                z[:],
-                nb_ps[:, half * HALF : (half + 1) * HALF].rearrange("p (n t) -> p n t", t=D),
-                src[half][:].unsqueeze(2).to_broadcast(by_node),
-                ALU.add,
-            )
-            e = held.tile(by_node, F32, name="e" + of_half)
-            nc.vector.scalar_tensor_tensor(e[:], z[:], SLOPE, z[:], ALU.mult, ALU.max)
+            z = z_ps[:, half * HALF : (half + 1) * HALF].rearrange("p (n t) -> p n t", t=D)
+            z_max = held.tile([P, HALF_NODES], F32, name="z_max" + of_half)
+            nc.vector.tensor_reduce(z_max[:], z, X, ALU.max)
+            z_low = held.tile(by_node, F32, name="z_low" + of_half)
+            nc.vector.tensor_scalar_mul(z_low[:], z, SLOPE)
             e_max = held.tile([P, HALF_NODES], F32, name="e_max" + of_half)
-            nc.vector.tensor_reduce(e_max[:], e[:], X, ALU.max)
+            nc.vector.scalar_tensor_tensor(e_max[:], z_max[:], SLOPE, z_max[:], ALU.mult, ALU.max)
+            e = held.tile(by_node, F32, name="e" + of_half)
+            nc.vector.tensor_tensor(e[:], z, z_low[:], ALU.max)
             shifted = held.tile(by_node, F32, name="shifted" + of_half)
             nc.vector.tensor_tensor(shifted[:], e[:], e_max[:].unsqueeze(2).to_broadcast(by_node), ALU.subtract)
             p_exp = held.tile(by_node, F32, name="p_exp" + of_half)

@@ -37,8 +37,7 @@ def tile_multihead_gaatn_kernel(tc, table, w, a1, a2, offs, out):
     with (
         tc.tile_pool(name="held", bufs=1) as held,
         tc.tile_pool(name="ring", bufs=3) as ring,
-        tc.psum_pool(name="bank_psum", bufs=1) as bank_psum,
-        tc.psum_pool(name="att_psum", bufs=4) as att_psum,
+        tc.psum_pool(name="bank_psum", bufs=8) as bank_psum,
     ):
         w_sb = held.tile([P, H * P], BF16, name="w_sb")
         nc.scalar.dma_start(w_sb[:], w)
@@ -101,8 +100,8 @@ def tile_multihead_gaatn_kernel(tc, table, w, a1, a2, offs, out):
                 vectors[:].unsqueeze(1).to_broadcast([P, TERMS, H]),
             )
 
-        banks = [bank_psum.tile([P, PIECE], F32, name="bank" + str(i)) for i in range(3)]
-        z_ps = banks[2][:, 0:BLOCK]
+        z_bank = bank_psum.tile([P, PIECE], F32, name="z_bank", tag="bank")
+        z_ps = z_bank[:, 0:BLOCK]
         for b in range(N_BLOCKS):
             nc.tensor.matmul(
                 z_ps.rearrange("p (n t) -> p n t", t=D),
@@ -161,7 +160,7 @@ def tile_multihead_gaatn_kernel(tc, table, w, a1, a2, offs, out):
         piece_cols = PIECE // PER_COL
         for k in range(H):
             for h in range(N_PIECES):
-                whj_ps = banks[(k * N_PIECES + h) % 3]
+                whj_ps = bank_psum.tile([P, PIECE], F32, name="whj_ps", tag="bank")
                 nc.tensor.matmul(
                     whj_ps[:],
                     w_sb[:, k * P : (k + 1) * P],
@@ -174,7 +173,7 @@ def tile_multihead_gaatn_kernel(tc, table, w, a1, a2, offs, out):
         agg = held.tile([P, H, N_BLOCKS, BLOCK_NODES], F32, name="agg")
 
         def spread_att(half, k):
-            att_ps = att_psum.tile([P, N_BLOCKS, HALF], F32, name="att_ps")
+            att_ps = bank_psum.tile([P, N_BLOCKS, HALF], F32, name="att_ps", tag="bank")
             for b in range(N_BLOCKS):
                 nc.tensor.matmul(att_ps[:, b, :], select[:, H * b + k, :], terms[half][:], start=True, stop=True)
             return att_ps

@@ -22,6 +22,9 @@ BLOCK_NODES = BLOCK // D
 HALVES = 2
 HALF_NODES = BLOCK_NODES // HALVES
 HALF = HALF_NODES * D
+CHAINS = 4
+CHAIN_NODES = BLOCK_NODES // CHAINS
+CHAIN = CHAIN_NODES * D
 ROWS = N_BLOCKS * H
 TERMS = 3
 GROUP = 32
@@ -120,41 +123,42 @@ def tile_multihead_gaatn_kernel(tc, table, w, a1, a2, offs, out):
                 stop=(b == N_BLOCKS - 1),
             )
 
-        by_node = [P, HALF_NODES, D]
-        terms = []
-        for half in range(HALVES):
-            of_half = str(half)
-            z = z_ps[:, half * HALF : (half + 1) * HALF].rearrange("p (n t) -> p n t", t=D)
-            z_max = held.tile([P, HALF_NODES], F32, name="z_max" + of_half)
+        by_node = [P, CHAIN_NODES, D]
+        terms = [held.tile([P, HALF], BF16, name="term" + str(half)) for half in range(HALVES)]
+        for chain in range(CHAINS):
+            of_chain = str(chain)
+            z = z_ps[:, chain * CHAIN : (chain + 1) * CHAIN].rearrange("p (n t) -> p n t", t=D)
+            z_max = held.tile([P, CHAIN_NODES], F32, name="z_max" + of_chain)
             nc.vector.tensor_reduce(z_max[:], z, X, ALU.max)
-            z_low = held.tile(by_node, F32, name="z_low" + of_half)
+            z_low = held.tile(by_node, F32, name="z_low" + of_chain)
             nc.vector.tensor_scalar_mul(z_low[:], z, SLOPE)
-            e_max = held.tile([P, HALF_NODES], F32, name="e_max" + of_half)
+            e_max = held.tile([P, CHAIN_NODES], F32, name="e_max" + of_chain)
             nc.vector.scalar_tensor_tensor(e_max[:], z_max[:], SLOPE, z_max[:], ALU.mult, ALU.max)
-            e = held.tile(by_node, F32, name="e" + of_half)
+            e = held.tile(by_node, F32, name="e" + of_chain)
             nc.vector.tensor_tensor(e[:], z, z_low[:], ALU.max)
-            shifted = held.tile(by_node, F32, name="shifted" + of_half)
+            shifted = held.tile(by_node, F32, name="shifted" + of_chain)
             nc.vector.tensor_tensor(shifted[:], e[:], e_max[:].unsqueeze(2).to_broadcast(by_node), ALU.subtract)
-            p_exp = held.tile(by_node, F32, name="p_exp" + of_half)
+            p_exp = held.tile(by_node, F32, name="p_exp" + of_chain)
             nc.scalar.activation(p_exp[:], shifted[:], ACT.Exp)
-            p_sum = held.tile([P, HALF_NODES], F32, name="p_sum" + of_half)
+            p_sum = held.tile([P, CHAIN_NODES], F32, name="p_sum" + of_chain)
             nc.vector.tensor_reduce(p_sum[:], p_exp[:], X, ALU.add)
-            p_inv = held.tile([P, HALF_NODES], F32, name="p_inv" + of_half)
+            p_inv = held.tile([P, CHAIN_NODES], F32, name="p_inv" + of_chain)
             nc.vector.reciprocal(p_inv[:], p_sum[:])
-            att = held.tile(by_node, F32, name="att" + of_half)
+            att = held.tile(by_node, F32, name="att" + of_chain)
             nc.vector.tensor_tensor(att[:], p_exp[:], p_inv[:].unsqueeze(2).to_broadcast(by_node), ALU.mult)
-            hi = held.tile(by_node, BF16, name="hi" + of_half)
+            hi = held.tile(by_node, BF16, name="hi" + of_chain)
             nc.vector.tensor_tensor(hi[:], p_exp[:], p_inv[:].unsqueeze(2).to_broadcast(by_node), ALU.mult)
 
             att_flat = att[:].rearrange("p n t -> p (n t)")
             hi_flat = hi[:].rearrange("p n t -> p (n t)")
-            rest = held.tile([P, HALF], F32, name="rest" + of_half)
+            rest = held.tile([P, CHAIN], F32, name="rest" + of_chain)
             nc.vector.scalar_tensor_tensor(rest[:], hi_flat, minus_hi[:], att_flat, ALU.mult, ALU.add)
-            rest_bf = held.tile([P, HALF], BF16, name="rest_bf" + of_half)
+            rest_bf = held.tile([P, CHAIN], BF16, name="rest_bf" + of_chain)
             nc.vector.scalar_tensor_tensor(rest_bf[:], hi_flat, minus_hi[:], att_flat, ALU.mult, ALU.add)
-            term = held.tile([P, HALF], BF16, name="term" + of_half)
-            nc.vector.scalar_tensor_tensor(term[:], rest_bf[:], minus_mid[:], rest[:], ALU.mult, ALU.add)
-            terms.append(term)
+            half, part = divmod(chain, CHAINS // HALVES)
+            nc.vector.scalar_tensor_tensor(
+                terms[half][:, part * CHAIN : (part + 1) * CHAIN], rest_bf[:], minus_mid[:], rest[:], ALU.mult, ALU.add
+            )
 
         whj = held.tile([P, H, N], F32, name="whj")
         piece_cols = PIECE // PER_COL

@@ -1,4 +1,5 @@
 import concourse.mybir as mybir
+from concourse.masks import make_identity
 
 F32 = mybir.dt.float32
 BF16 = mybir.dt.bfloat16
@@ -40,7 +41,8 @@ def tile_multihead_gaatn_kernel(tc, table, w, a1, a2, offs, out):
     with (
         tc.tile_pool(name="held", bufs=1) as held,
         tc.tile_pool(name="ring", bufs=3) as ring,
-        tc.psum_pool(name="bank_psum", bufs=8) as bank_psum,
+        tc.psum_pool(name="bank_psum", bufs=7) as bank_psum,
+        tc.psum_pool(name="sum_psum", bufs=1) as sum_psum,
     ):
         w_sb = held.tile([P, H * P], BF16, name="w_sb")
         nc.scalar.dma_start(w_sb[:], w)
@@ -81,6 +83,28 @@ def tile_multihead_gaatn_kernel(tc, table, w, a1, a2, offs, out):
             )
         select = held.tile([P, ROWS, P], BF16, name="select")
         nc.gpsimd.tensor_scalar(select[:], picks[:].unsqueeze(2).to_broadcast([P, ROWS, P]), 1.0, 0.0, ALU.mult, ALU.add)
+        identity = held.tile([P, P], F32, name="identity")
+        make_identity(nc, identity[:])
+        same_node = held.tile([P, HALF_NODES], F32, name="same_node")
+        nc.gpsimd.memset(same_node[:], 1.0)
+        nc.gpsimd.affine_select(
+            out=same_node[:],
+            in_=same_node[:],
+            pattern=[[-D, HALF_NODES]],
+            compare_op=ALU.is_ge,
+            fill=0.0,
+            base=0,
+            channel_multiplier=1,
+        )
+        nc.gpsimd.affine_select(
+            out=same_node[:],
+            in_=same_node[:],
+            pattern=[[D, HALF_NODES]],
+            compare_op=ALU.is_ge,
+            fill=0.0,
+            base=D - 1,
+            channel_multiplier=-1,
+        )
         minus_hi = held.tile([P, 1], F32, name="minus_hi")
         nc.vector.memset(minus_hi[0:GROUP, :], 0.0)
         nc.vector.memset(minus_hi[GROUP : 2 * GROUP, :], -1.0)
@@ -125,6 +149,7 @@ def tile_multihead_gaatn_kernel(tc, table, w, a1, a2, offs, out):
 
         by_node = [P, CHAIN_NODES, D]
         terms = [held.tile([P, HALF], BF16, name="term" + str(half)) for half in range(HALVES)]
+        att_rows = [held.tile([P, HALF], F32, name="att_rows" + str(half)) for half in range(HALVES)]
         for chain in range(CHAINS):
             of_chain = str(chain)
             z = z_ps[:, chain * CHAIN : (chain + 1) * CHAIN].rearrange("p (n t) -> p n t", t=D)
@@ -144,18 +169,22 @@ def tile_multihead_gaatn_kernel(tc, table, w, a1, a2, offs, out):
             nc.vector.tensor_reduce(p_sum[:], p_exp[:], X, ALU.add)
             p_inv = held.tile([P, CHAIN_NODES], F32, name="p_inv" + of_chain)
             nc.vector.reciprocal(p_inv[:], p_sum[:])
-            att = held.tile(by_node, F32, name="att" + of_chain)
-            nc.vector.tensor_tensor(att[:], p_exp[:], p_inv[:].unsqueeze(2).to_broadcast(by_node), ALU.mult)
+            half, part = divmod(chain, CHAINS // HALVES)
+            att_flat = att_rows[half][:, part * CHAIN : (part + 1) * CHAIN]
+            nc.vector.tensor_tensor(
+                att_flat.rearrange("p (n t) -> p n t", t=D),
+                p_exp[:],
+                p_inv[:].unsqueeze(2).to_broadcast(by_node),
+                ALU.mult,
+            )
             hi = held.tile(by_node, BF16, name="hi" + of_chain)
             nc.vector.tensor_tensor(hi[:], p_exp[:], p_inv[:].unsqueeze(2).to_broadcast(by_node), ALU.mult)
 
-            att_flat = att[:].rearrange("p n t -> p (n t)")
             hi_flat = hi[:].rearrange("p n t -> p (n t)")
             rest = held.tile([P, CHAIN], F32, name="rest" + of_chain)
             nc.vector.scalar_tensor_tensor(rest[:], hi_flat, minus_hi[:], att_flat, ALU.mult, ALU.add)
             rest_bf = held.tile([P, CHAIN], BF16, name="rest_bf" + of_chain)
             nc.vector.scalar_tensor_tensor(rest_bf[:], hi_flat, minus_hi[:], att_flat, ALU.mult, ALU.add)
-            half, part = divmod(chain, CHAINS // HALVES)
             nc.vector.scalar_tensor_tensor(
                 terms[half][:, part * CHAIN : (part + 1) * CHAIN], rest_bf[:], minus_mid[:], rest[:], ALU.mult, ALU.add
             )
@@ -185,34 +214,68 @@ def tile_multihead_gaatn_kernel(tc, table, w, a1, a2, offs, out):
         def whj_of(half, k):
             return whj[:, k, :].rearrange("p (b c) -> p b c", c=BLOCK)[:, :, half * HALF : (half + 1) * HALF]
 
-        def sum_neighbours(half, k, weighted):
-            nc.vector.tensor_reduce(agg[:, k, :, half * HALF_NODES : (half + 1) * HALF_NODES], weighted[:], X, ALU.add)
-            if half == HALVES - 1:
-                result = held.tile([P, P], F32, name="result" + str(k))
-                nc.scalar.activation(result[:], agg[:, k, :, :].rearrange("p b n -> p (b n)"), ACT.Relu)
-                queue = nc.sync if k % 2 == 0 else nc.scalar
-                queue.dma_start(out[k * P : (k + 1) * P, :], result[:])
+        def multiply_on_vector(half, k):
+            att_ps = spread_att(half, k)
+            weighted = ring.tile([P, N_BLOCKS, HALF_NODES, D], F32, name="weighted")
+            nc.vector.tensor_tensor(weighted[:].rearrange("p b n t -> p b (n t)"), att_ps[:], whj_of(half, k), ALU.mult)
+            return weighted
 
         def multiply_on_gpsimd(half, k):
             att_ps = spread_att(half, k)
             att_sb = ring.tile([P, N_BLOCKS, HALF], F32, name="att_sb")
             nc.scalar.copy(att_sb[:], att_ps[:])
-            weighted = held.tile([P, N_BLOCKS, HALF_NODES, D], F32, name="weighted_g" + str(half) + str(k))
+            weighted = ring.tile([P, N_BLOCKS, HALF_NODES, D], F32, name="weighted_g")
             nc.gpsimd.tensor_tensor(weighted[:].rearrange("p b n t -> p b (n t)"), att_sb[:], whj_of(half, k), ALU.mult)
             return half, k, weighted
 
+        def finish(k, sums):
+            result = held.tile([P, P], F32, name="result" + str(k))
+            nc.scalar.activation(result[:], sums.rearrange("p b n -> p (b n)"), ACT.Relu)
+            queue = nc.sync if k % 2 == 0 else nc.scalar
+            queue.dma_start(out[k * P : (k + 1) * P, :], result[:])
+
+        units_left = {k: HALVES for k in range(H)}
+
+        def sum_neighbours(half, k, weighted):
+            nc.vector.tensor_reduce(agg[:, k, :, half * HALF_NODES : (half + 1) * HALF_NODES], weighted[:], X, ALU.add)
+            units_left[k] = units_left[k] - 1
+            if units_left[k] == 0:
+                finish(k, agg[:, k, :, :])
+
+        def sum_transposed(k):
+            agg_ps = sum_psum.tile([P, N_BLOCKS, BLOCK_NODES], F32, name="agg_ps")
+            for half in range(HALVES):
+                att_cols_ps = bank_psum.tile([P, P], F32, name="att_cols_ps", tag="bank")
+                nc.tensor.transpose(att_cols_ps[:], att_rows[half][:], identity[:])
+                att_cols = held.tile([P, ROWS], F32, name="att_cols" + str(half))
+                nc.scalar.copy(att_cols[:], att_cols_ps[:, 0:ROWS])
+                whj_t_ps = bank_psum.tile([P, N_BLOCKS, P], F32, name="whj_t_ps", tag="bank")
+                for b in range(N_BLOCKS):
+                    first = b * BLOCK + half * HALF
+                    nc.tensor.transpose(whj_t_ps[:, b, :], whj[:, k, first : first + HALF], identity[:])
+                for b in range(N_BLOCKS):
+                    scaled = ring.tile([P, P], F32, name="scaled")
+                    nc.scalar.activation(
+                        scaled[:], whj_t_ps[:, b, :], ACT.Copy, scale=att_cols[:, H * b + k : H * b + k + 1]
+                    )
+                    nc.tensor.matmul(
+                        agg_ps[:, b, half * HALF_NODES : (half + 1) * HALF_NODES],
+                        scaled[:],
+                        same_node[:],
+                        start=True,
+                        stop=True,
+                    )
+            finish(k, agg_ps[:])
+
         unsummed = []
         for half in range(HALVES):
-            started = [multiply_on_gpsimd(half, k) for k in range(H - GPSIMD_HEADS, H)]
-            for k in range(H - GPSIMD_HEADS):
-                att_ps = spread_att(half, k)
-                weighted = ring.tile([P, N_BLOCKS, HALF_NODES, D], F32, name="weighted")
-                nc.vector.tensor_tensor(
-                    weighted[:].rearrange("p b n t -> p b (n t)"), att_ps[:], whj_of(half, k), ALU.mult
-                )
-                sum_neighbours(half, k, weighted)
+            first_gpsimd_head = H - GPSIMD_HEADS + half
+            started = [multiply_on_gpsimd(half, k) for k in range(first_gpsimd_head, H)]
+            for k in range(1, first_gpsimd_head):
+                sum_neighbours(half, k, multiply_on_vector(half, k))
             for earlier_half, k, weighted in unsummed:
                 sum_neighbours(earlier_half, k, weighted)
             unsummed = started
+        sum_transposed(0)
         for last_half, k, weighted in unsummed:
             sum_neighbours(last_half, k, weighted)

@@ -203,6 +203,14 @@ def tile_multihead_gaatn_kernel(tc, table, w, a1, a2, offs, out):
                 )
                 nc.scalar.copy(whj[:, k, h * PIECE : (h + 1) * PIECE], whj_ps[:])
 
+        att_cols = []
+        for half in range(HALVES):
+            att_cols_ps = bank_psum.tile([P, P], F32, name="att_cols_ps", tag="bank")
+            nc.tensor.transpose(att_cols_ps[:], att_rows[half][:], identity[:])
+            att_cols_half = held.tile([P, ROWS], F32, name="att_cols" + str(half))
+            nc.scalar.copy(att_cols_half[:], att_cols_ps[:, 0:ROWS])
+            att_cols.append(att_cols_half)
+
         agg = held.tile([P, H, N_BLOCKS, BLOCK_NODES], F32, name="agg")
 
         def spread_att(half, k):
@@ -245,10 +253,6 @@ def tile_multihead_gaatn_kernel(tc, table, w, a1, a2, offs, out):
         def sum_transposed(k):
             agg_ps = sum_psum.tile([P, N_BLOCKS, BLOCK_NODES], F32, name="agg_ps")
             for half in range(HALVES):
-                att_cols_ps = bank_psum.tile([P, P], F32, name="att_cols_ps", tag="bank")
-                nc.tensor.transpose(att_cols_ps[:], att_rows[half][:], identity[:])
-                att_cols = held.tile([P, ROWS], F32, name="att_cols" + str(half))
-                nc.scalar.copy(att_cols[:], att_cols_ps[:, 0:ROWS])
                 whj_t_ps = bank_psum.tile([P, N_BLOCKS, P], F32, name="whj_t_ps", tag="bank")
                 for b in range(N_BLOCKS):
                     first = b * BLOCK + half * HALF
@@ -256,7 +260,7 @@ def tile_multihead_gaatn_kernel(tc, table, w, a1, a2, offs, out):
                 for b in range(N_BLOCKS):
                     scaled = ring.tile([P, P], F32, name="scaled")
                     nc.scalar.activation(
-                        scaled[:], whj_t_ps[:, b, :], ACT.Copy, scale=att_cols[:, H * b + k : H * b + k + 1]
+                        scaled[:], whj_t_ps[:, b, :], ACT.Copy, scale=att_cols[half][:, H * b + k : H * b + k + 1]
                     )
                     nc.tensor.matmul(
                         agg_ps[:, b, half * HALF_NODES : (half + 1) * HALF_NODES],

@@ -17,21 +17,9 @@ SLOPE = 0.01
 
 PIECE = 512
 N_PIECES = N // PIECE
-BLOCK = 256
-N_BLOCKS = N // BLOCK
-BLOCK_NODES = BLOCK // D
-HALVES = 2
-HALF_NODES = BLOCK_NODES // HALVES
-HALF = HALF_NODES * D
-CHAINS = 4
-CHAIN_NODES = BLOCK_NODES // CHAINS
-CHAIN = CHAIN_NODES * D
-ROWS = N_BLOCKS * H
-TERMS = 3
-GROUP = 32
-SHIFT = H * (N_BLOCKS - 1)
 PER_COL = 16
-GPSIMD_HEADS = 2
+SCORE_ROWS = 64
+PER_BANK = PIECE // P
 
 FLOPS = 2 * P * (H * P) * (N + P)
 
@@ -40,246 +28,131 @@ def tile_multihead_gaatn_kernel(tc, table, w, a1, a2, offs, out):
     nc = tc.nc
     with (
         tc.tile_pool(name="held", bufs=1) as held,
-        tc.tile_pool(name="ring", bufs=3) as ring,
-        tc.psum_pool(name="bank_psum", bufs=7) as bank_psum,
-        tc.psum_pool(name="sum_psum", bufs=1) as sum_psum,
+        tc.tile_pool(name="ring", bufs=4) as ring,
+        tc.psum_pool(name="bank_psum", bufs=8) as bank_psum,
     ):
         w_sb = held.tile([P, H * P], BF16, name="w_sb")
         nc.scalar.dma_start(w_sb[:], w)
-        a1_all = held.tile([P, H * P], F32, name="a1_all")
-        nc.sync.dma_start(a1_all[:], a1.rearrange("c o -> (c o)").partition_broadcast(P))
         a2_all = held.tile([P, H * P], F32, name="a2_all")
-        nc.scalar.dma_start(a2_all[:], a2.rearrange("c o -> (c o)").partition_broadcast(P))
-        offsets = held.tile([P, N // PER_COL], U16, name="offsets")
-        nc.sync.dma_start(offsets[:], offs)
+        nc.sync.dma_start(a2_all[:], a2.rearrange("c o -> (c o)").partition_broadcast(P))
         table_sb = held.tile([P, S], BF16, name="table_sb")
+        offsets = held.tile([P, N // PER_COL], U16, name="offsets")
+        a1_all = held.tile([P, H * P], F32, name="a1_all")
         chunk = S // 4
         for c in range(4):
-            queue = nc.sync if c % 2 == 0 else nc.scalar
+            queue = nc.scalar if c % 2 == 0 else nc.sync
             queue.dma_start(table_sb[:, c * chunk : (c + 1) * chunk], table[:, c * chunk : (c + 1) * chunk])
+            if c == 0:
+                nc.sync.dma_start(offsets[:], offs)
+        nc.sync.dma_start(a1_all[:], a1.rearrange("c o -> (c o)").partition_broadcast(P))
 
         warm = held.tile([P, 1], F32, name="warm")
         nc.vector.memset(warm[:], 0.0)
         nc.scalar.activation(warm[:], warm[:], ACT.Exp)
-        u_weights = held.tile([P, SHIFT + P], BF16, name="u_weights")
-        nc.gpsimd.memset(u_weights[:], 0.0)
-        v_weights = held.tile([P, SHIFT + P], BF16, name="v_weights")
+        v_weights = held.tile([P, P], BF16, name="v_weights")
         nc.gpsimd.memset(v_weights[:], 0.0)
-
-        def weights_of_block(weights, b):
-            return weights[:, SHIFT - H * b : SHIFT - H * b + P]
-
-        picks = held.tile([P, ROWS], F32, name="picks")
-        nc.gpsimd.memset(picks[:], 0.0)
-        for g in range(TERMS):
-            nc.gpsimd.affine_select(
-                out=picks[:],
-                in_=picks[:],
-                pattern=[[-1, ROWS]],
-                compare_op=ALU.not_equal,
-                fill=1.0,
-                base=-GROUP * g,
-                channel_multiplier=1,
-            )
-        select = held.tile([P, ROWS, P], BF16, name="select")
-        nc.gpsimd.tensor_scalar(select[:], picks[:].unsqueeze(2).to_broadcast([P, ROWS, P]), 1.0, 0.0, ALU.mult, ALU.add)
         identity = held.tile([P, P], F32, name="identity")
         make_identity(nc, identity[:])
-        same_node = held.tile([P, HALF_NODES], F32, name="same_node")
-        nc.gpsimd.memset(same_node[:], 1.0)
-        nc.gpsimd.affine_select(
-            out=same_node[:],
-            in_=same_node[:],
-            pattern=[[-D, HALF_NODES]],
-            compare_op=ALU.is_ge,
-            fill=0.0,
-            base=0,
-            channel_multiplier=1,
-        )
-        nc.gpsimd.affine_select(
-            out=same_node[:],
-            in_=same_node[:],
-            pattern=[[D, HALF_NODES]],
-            compare_op=ALU.is_ge,
-            fill=0.0,
-            base=D - 1,
-            channel_multiplier=-1,
-        )
-        minus_hi = held.tile([P, 1], F32, name="minus_hi")
-        nc.vector.memset(minus_hi[0:GROUP, :], 0.0)
-        nc.vector.memset(minus_hi[GROUP : 2 * GROUP, :], -1.0)
-        nc.vector.memset(minus_hi[2 * GROUP : P, :], -1.0)
-        minus_mid = held.tile([P, 1], F32, name="minus_mid")
-        nc.vector.memset(minus_mid[0 : 2 * GROUP, :], 0.0)
-        nc.vector.memset(minus_mid[2 * GROUP : P, :], -1.0)
 
-        u = held.tile([P, H], F32, name="u")
-        v = held.tile([P, H], F32, name="v")
-        for a_all, vectors, weights in ((a1_all, u, u_weights), (a2_all, v, v_weights)):
+        def dot_with_row(sums, rows, row):
             for k in range(H):
                 head = slice(k * P, (k + 1) * P)
                 products = ring.tile([P, P], F32, name="products")
                 nc.vector.scalar_tensor_tensor(
-                    products[:], w_sb[:, head], 1.0, a_all[:, head], ALU.mult, ALU.mult, accum_out=vectors[:, k : k + 1]
+                    products[:], rows[:, head], 1.0, row[:, head], ALU.mult, ALU.mult, accum_out=sums[:, k : k + 1]
                 )
-            nc.vector.tensor_copy(
-                weights[:, SHIFT : SHIFT + TERMS * GROUP].rearrange("p (g y) -> p g y", y=GROUP)[:, :, 0:H],
-                vectors[:].unsqueeze(1).to_broadcast([P, TERMS, H]),
-            )
 
-        z_bank = bank_psum.tile([P, PIECE], F32, name="z_bank", tag="bank")
-        z_ps = z_bank[:, 0:BLOCK]
-        for b in range(N_BLOCKS):
-            nc.tensor.matmul(
-                z_ps.rearrange("p (n t) -> p n t", t=D),
-                weights_of_block(u_weights, b),
-                table_sb[:, b * BLOCK_NODES : (b + 1) * BLOCK_NODES].unsqueeze(2).to_broadcast([P, BLOCK_NODES, D]),
-                start=(b == 0),
-                stop=False,
-            )
-        block_cols = BLOCK // PER_COL
-        for b in range(N_BLOCKS):
-            nc.tensor.matmul(
-                z_ps,
-                weights_of_block(v_weights, b),
-                table_sb[:].indirect(offsets[:, b * block_cols : (b + 1) * block_cols]),
-                start=False,
-                stop=(b == N_BLOCKS - 1),
-            )
+        v = held.tile([P, H], F32, name="v")
+        dot_with_row(v, w_sb, a2_all)
+        nc.vector.tensor_scalar_mul(v_weights[:, 0:H], v[:], -1.0)
 
-        by_node = [P, CHAIN_NODES, D]
-        terms = [held.tile([P, HALF], BF16, name="term" + str(half)) for half in range(HALVES)]
-        att_rows = [held.tile([P, HALF], F32, name="att_rows" + str(half)) for half in range(HALVES)]
-        for chain in range(CHAINS):
-            of_chain = str(chain)
-            z = z_ps[:, chain * CHAIN : (chain + 1) * CHAIN].rearrange("p (n t) -> p n t", t=D)
-            z_max = held.tile([P, CHAIN_NODES], F32, name="z_max" + of_chain)
-            nc.vector.tensor_reduce(z_max[:], z, X, ALU.max)
-            z_low = held.tile(by_node, F32, name="z_low" + of_chain)
-            nc.vector.tensor_scalar_mul(z_low[:], z, SLOPE)
-            e_max = held.tile([P, CHAIN_NODES], F32, name="e_max" + of_chain)
-            nc.vector.scalar_tensor_tensor(e_max[:], z_max[:], SLOPE, z_max[:], ALU.mult, ALU.max)
-            e = held.tile(by_node, F32, name="e" + of_chain)
-            nc.vector.tensor_tensor(e[:], z, z_low[:], ALU.max)
-            shifted = held.tile(by_node, F32, name="shifted" + of_chain)
-            nc.vector.tensor_tensor(shifted[:], e[:], e_max[:].unsqueeze(2).to_broadcast(by_node), ALU.subtract)
-            p_exp = held.tile(by_node, F32, name="p_exp" + of_chain)
-            nc.scalar.activation(p_exp[:], shifted[:], ACT.Exp)
-            p_sum = held.tile([P, CHAIN_NODES], F32, name="p_sum" + of_chain)
-            nc.vector.tensor_reduce(p_sum[:], p_exp[:], X, ALU.add)
-            p_inv = held.tile([P, CHAIN_NODES], F32, name="p_inv" + of_chain)
-            nc.vector.reciprocal(p_inv[:], p_sum[:])
-            half, part = divmod(chain, CHAINS // HALVES)
-            att_flat = att_rows[half][:, part * CHAIN : (part + 1) * CHAIN]
-            nc.vector.tensor_tensor(
-                att_flat.rearrange("p (n t) -> p n t", t=D),
-                p_exp[:],
-                p_inv[:].unsqueeze(2).to_broadcast(by_node),
-                ALU.mult,
-            )
-            hi = held.tile(by_node, BF16, name="hi" + of_chain)
-            nc.vector.tensor_tensor(hi[:], p_exp[:], p_inv[:].unsqueeze(2).to_broadcast(by_node), ALU.mult)
+        whd_ps = bank_psum.tile([P, H * P], F32, name="whd_ps", tag="bank")
+        nc.tensor.matmul(whd_ps[:], table_sb[:, 0:P], w_sb[:], start=True, stop=True)
+        src = held.tile([P, H], F32, name="src")
+        dot_with_row(src, whd_ps, a1_all)
 
-            hi_flat = hi[:].rearrange("p n t -> p (n t)")
-            rest = held.tile([P, CHAIN], F32, name="rest" + of_chain)
-            nc.vector.scalar_tensor_tensor(rest[:], hi_flat, minus_hi[:], att_flat, ALU.mult, ALU.add)
-            rest_bf = held.tile([P, CHAIN], BF16, name="rest_bf" + of_chain)
-            nc.vector.scalar_tensor_tensor(rest_bf[:], hi_flat, minus_hi[:], att_flat, ALU.mult, ALU.add)
-            nc.vector.scalar_tensor_tensor(
-                terms[half][:, part * CHAIN : (part + 1) * CHAIN], rest_bf[:], minus_mid[:], rest[:], ALU.mult, ALU.add
-            )
+        piece_cols = PIECE // PER_COL
+
+        def looked_up(h):
+            return table_sb[:].indirect(offsets[:, h * piece_cols : (h + 1) * piece_cols])
+
+        nb = held.tile([SCORE_ROWS, N], F32, name="nb")
+        for h in range(N_PIECES):
+            nb_ps = bank_psum.tile([P, PIECE], F32, name="nb_ps", tag="bank")
+            nc.tensor.matmul(nb_ps[:], v_weights[:], looked_up(h), start=True, stop=True)
+            piece = slice(h * PIECE, (h + 1) * PIECE)
+            if h % 2 == 0:
+                nc.scalar.copy(nb[:, piece], nb_ps[0:SCORE_ROWS, :])
+            else:
+                nc.vector.tensor_copy(nb[:, piece], nb_ps[0:SCORE_ROWS, :])
 
         whj = held.tile([P, H, N], F32, name="whj")
-        piece_cols = PIECE // PER_COL
-        for k in range(H):
+
+        def project(k):
             for h in range(N_PIECES):
                 whj_ps = bank_psum.tile([P, PIECE], F32, name="whj_ps", tag="bank")
-                nc.tensor.matmul(
-                    whj_ps[:],
-                    w_sb[:, k * P : (k + 1) * P],
-                    table_sb[:].indirect(offsets[:, h * piece_cols : (h + 1) * piece_cols]),
-                    start=True,
-                    stop=True,
-                )
+                nc.tensor.matmul(whj_ps[:], w_sb[:, k * P : (k + 1) * P], looked_up(h), start=True, stop=True)
                 nc.scalar.copy(whj[:, k, h * PIECE : (h + 1) * PIECE], whj_ps[:])
 
-        att_cols = []
-        for half in range(HALVES):
-            att_cols_ps = bank_psum.tile([P, P], F32, name="att_cols_ps", tag="bank")
-            nc.tensor.transpose(att_cols_ps[:], att_rows[half][:], identity[:])
-            att_cols_half = held.tile([P, ROWS], F32, name="att_cols" + str(half))
-            nc.scalar.copy(att_cols_half[:], att_cols_ps[:, 0:ROWS])
-            att_cols.append(att_cols_half)
+        def turn(k):
+            slices = []
+            for first in range(0, D, PER_BANK):
+                bank = bank_psum.tile([P, PER_BANK, P], F32, name="slices_ps", tag="bank")
+                for t in range(first, first + PER_BANK):
+                    nc.tensor.transpose(bank[:, t - first, :], whj[:, k, t::D], identity[:])
+                slices.append(bank)
+            return slices
 
-        agg = held.tile([P, H, N_BLOCKS, BLOCK_NODES], F32, name="agg")
+        project(0)
+        nb_t_ps = bank_psum.tile([P, D, SCORE_ROWS], F32, name="nb_t_ps", tag="bank")
+        for t in range(D):
+            nc.tensor.transpose(nb_t_ps[:, t, :], nb[:, t::D], identity[0:SCORE_ROWS, 0:SCORE_ROWS])
+        slices_of = []
+        for k in range(1, H):
+            project(k)
+            slices_of.append(turn(k - 1))
+        slices_of.append(turn(H - 1))
 
-        def spread_att(half, k):
-            att_ps = bank_psum.tile([P, N_BLOCKS, HALF], F32, name="att_ps", tag="bank")
-            for b in range(N_BLOCKS):
-                nc.tensor.matmul(att_ps[:, b, :], select[:, H * b + k, :], terms[half][:], start=True, stop=True)
-            return att_ps
+        by_node = [P, H, D]
+        z_neg = held.tile(by_node, F32, name="z_neg")
+        nc.vector.tensor_tensor(
+            z_neg[:],
+            nb_t_ps[:, :, 0:H].rearrange("p t k -> p k t"),
+            src[:].unsqueeze(2).to_broadcast(by_node),
+            ALU.subtract,
+        )
+        e_neg = held.tile(by_node, F32, name="e_neg")
+        nc.vector.scalar_tensor_tensor(e_neg[:], z_neg[:], SLOPE, z_neg[:], ALU.mult, ALU.min)
+        e_max_neg = held.tile([P, H], F32, name="e_max_neg")
+        nc.vector.tensor_reduce(e_max_neg[:], e_neg[:], X, ALU.min)
+        p_exp = held.tile(by_node, F32, name="p_exp")
+        p_sum = held.tile([P, H], F32, name="p_sum")
+        for k in range(H):
+            nc.scalar.activation(
+                p_exp[:, k, :], e_neg[:, k, :], ACT.Exp, bias=e_max_neg[:, k : k + 1], scale=-1.0, accum_out=p_sum[:, k : k + 1]
+            )
+        p_inv = held.tile([P, H], F32, name="p_inv")
+        nc.vector.reciprocal(p_inv[:], p_sum[:])
+        att = held.tile(by_node, F32, name="att")
+        nc.vector.tensor_tensor(att[:], p_exp[:], p_inv[:].unsqueeze(2).to_broadcast(by_node), ALU.mult)
 
-        def whj_of(half, k):
-            return whj[:, k, :].rearrange("p (b c) -> p b c", c=BLOCK)[:, :, half * HALF : (half + 1) * HALF]
-
-        def multiply_on_vector(half, k):
-            att_ps = spread_att(half, k)
-            weighted = ring.tile([P, N_BLOCKS, HALF_NODES, D], F32, name="weighted")
-            nc.vector.tensor_tensor(weighted[:].rearrange("p b n t -> p b (n t)"), att_ps[:], whj_of(half, k), ALU.mult)
-            return weighted
-
-        def multiply_on_gpsimd(half, k):
-            att_ps = spread_att(half, k)
-            att_sb = ring.tile([P, N_BLOCKS, HALF], F32, name="att_sb")
-            nc.scalar.copy(att_sb[:], att_ps[:])
-            weighted = ring.tile([P, N_BLOCKS, HALF_NODES, D], F32, name="weighted_g")
-            nc.gpsimd.tensor_tensor(weighted[:].rearrange("p b n t -> p b (n t)"), att_sb[:], whj_of(half, k), ALU.mult)
-            return half, k, weighted
-
-        def finish(k, sums):
-            result = held.tile([P, P], F32, name="result" + str(k))
-            nc.scalar.activation(result[:], sums.rearrange("p b n -> p (b n)"), ACT.Relu)
-            queue = nc.sync if k % 2 == 0 else nc.scalar
-            queue.dma_start(out[k * P : (k + 1) * P, :], result[:])
-
-        units_left = {k: HALVES for k in range(H)}
-
-        def sum_neighbours(half, k, weighted):
-            nc.vector.tensor_reduce(agg[:, k, :, half * HALF_NODES : (half + 1) * HALF_NODES], weighted[:], X, ALU.add)
-            units_left[k] = units_left[k] - 1
-            if units_left[k] == 0:
-                finish(k, agg[:, k, :, :])
-
-        def sum_transposed(k):
-            agg_ps = sum_psum.tile([P, N_BLOCKS, BLOCK_NODES], F32, name="agg_ps")
-            for half in range(HALVES):
-                whj_t_ps = bank_psum.tile([P, N_BLOCKS, P], F32, name="whj_t_ps", tag="bank")
-                for b in range(N_BLOCKS):
-                    first = b * BLOCK + half * HALF
-                    nc.tensor.transpose(whj_t_ps[:, b, :], whj[:, k, first : first + HALF], identity[:])
-                for b in range(N_BLOCKS):
-                    scaled = ring.tile([P, P], F32, name="scaled")
-                    nc.scalar.activation(
-                        scaled[:], whj_t_ps[:, b, :], ACT.Copy, scale=att_cols[half][:, H * b + k : H * b + k + 1]
-                    )
-                    nc.tensor.matmul(
-                        agg_ps[:, b, half * HALF_NODES : (half + 1) * HALF_NODES],
-                        scaled[:],
-                        same_node[:],
-                        start=True,
-                        stop=True,
-                    )
-            finish(k, agg_ps[:])
-
-        unsummed = []
-        for half in range(HALVES):
-            first_gpsimd_head = H - GPSIMD_HEADS + half
-            started = [multiply_on_gpsimd(half, k) for k in range(first_gpsimd_head, H)]
-            for k in range(1, first_gpsimd_head):
-                sum_neighbours(half, k, multiply_on_vector(half, k))
-            for earlier_half, k, weighted in unsummed:
-                sum_neighbours(earlier_half, k, weighted)
-            unsummed = started
-        sum_transposed(0)
-        for last_half, k, weighted in unsummed:
-            sum_neighbours(last_half, k, weighted)
+        half_bank = PER_BANK // 2
+        for k in range(H):
+            sums = [held.tile([P, P], F32, name="sum%d_%d" % (k, i)) for i in range(D // 2)]
+            for step in range(2):
+                for i in range(D // 2):
+                    t = (i // half_bank) * PER_BANK + PER_BANK - 1 - step * half_bank - i % half_bank
+                    piece = slices_of[k][t // PER_BANK][:, t % PER_BANK, :]
+                    weight = att[:, k, t : t + 1]
+                    if step == 0:
+                        nc.vector.tensor_scalar(sums[i][:], piece, weight, None, ALU.mult)
+                    else:
+                        nc.vector.scalar_tensor_tensor(sums[i][:], piece, weight, sums[i][:], ALU.mult, ALU.add)
+            result_ps = bank_psum.tile([P, PIECE], F32, name="result_ps", tag="bank")
+            for i in range(D // 2):
+                nc.tensor.matmul(
+                    result_ps[:, 0:P], sums[i][:], identity[:], start=(i == 0), stop=(i == D // 2 - 1), is_transpose=True
+                )
+            result = ring.tile([P, P], F32, name="result")
+            nc.scalar.activation(result[:], result_ps[:, 0:P], ACT.Relu)
+            nc.sync.dma_start(out[k * P : (k + 1) * P, :], result[:])

@@ -17,6 +17,7 @@ SLOPE = 0.01
 
 PIECE = 512
 N_PIECES = N // PIECE
+PIECE_NODES = PIECE // D
 PER_COL = 16
 SCORE_ROWS = 64
 PER_BANK = PIECE // P
@@ -76,37 +77,39 @@ def tile_multihead_gaatn_kernel(tc, table, w, a1, a2, offs, out):
         def looked_up(h):
             return table_sb[:].indirect(offsets[:, h * piece_cols : (h + 1) * piece_cols])
 
-        nb = held.tile([SCORE_ROWS, N], F32, name="nb")
+        nb = held.tile([SCORE_ROWS, D, P], F32, name="nb")
         for h in range(N_PIECES):
             nb_ps = bank_psum.tile([P, PIECE], F32, name="nb_ps", tag="bank")
             nc.tensor.matmul(nb_ps[:], v_weights[:], looked_up(h), start=True, stop=True)
-            piece = slice(h * PIECE, (h + 1) * PIECE)
+            by_slice = nb_ps[0:SCORE_ROWS, :].rearrange("p (n t) -> p t n", t=D)
+            nodes = slice(h * PIECE_NODES, (h + 1) * PIECE_NODES)
             if h % 2 == 0:
-                nc.scalar.copy(nb[:, piece], nb_ps[0:SCORE_ROWS, :])
+                nc.scalar.copy(nb[:, :, nodes], by_slice)
             else:
-                nc.vector.tensor_copy(nb[:, piece], nb_ps[0:SCORE_ROWS, :])
+                nc.vector.tensor_copy(nb[:, :, nodes], by_slice)
 
-        whj = held.tile([P, H, N], F32, name="whj")
+        whj = held.tile([P, H, D, P], F32, name="whj")
 
         def project(k):
             for h in range(N_PIECES):
                 whj_ps = bank_psum.tile([P, PIECE], F32, name="whj_ps", tag="bank")
                 nc.tensor.matmul(whj_ps[:], w_sb[:, k * P : (k + 1) * P], looked_up(h), start=True, stop=True)
-                nc.scalar.copy(whj[:, k, h * PIECE : (h + 1) * PIECE], whj_ps[:])
+                nodes = slice(h * PIECE_NODES, (h + 1) * PIECE_NODES)
+                nc.scalar.copy(whj[:, k, :, nodes], whj_ps[:].rearrange("p (n t) -> p t n", t=D))
 
         def turn(k):
             slices = []
             for first in range(0, D, PER_BANK):
                 bank = bank_psum.tile([P, PER_BANK, P], F32, name="slices_ps", tag="bank")
                 for t in range(first, first + PER_BANK):
-                    nc.tensor.transpose(bank[:, t - first, :], whj[:, k, t::D], identity[:])
+                    nc.tensor.transpose(bank[:, t - first, :], whj[:, k, t, :], identity[:])
                 slices.append(bank)
             return slices
 
         project(0)
         nb_t_ps = bank_psum.tile([P, D, SCORE_ROWS], F32, name="nb_t_ps", tag="bank")
         for t in range(D):
-            nc.tensor.transpose(nb_t_ps[:, t, :], nb[:, t::D], identity[0:SCORE_ROWS, 0:SCORE_ROWS])
+            nc.tensor.transpose(nb_t_ps[:, t, :], nb[:, t, :], identity[0:SCORE_ROWS, 0:SCORE_ROWS])
         slices_of = []
         for k in range(1, H):
             project(k)

@@ -90,12 +90,11 @@ def tile_multihead_gaatn_kernel(tc, table, w, a1, a2, offs, out):
 
         whj = held.tile([P, H, D, P], F32, name="whj")
 
-        def project(k):
-            for h in range(N_PIECES):
-                whj_ps = bank_psum.tile([P, PIECE], F32, name="whj_ps", tag="bank")
-                nc.tensor.matmul(whj_ps[:], w_sb[:, k * P : (k + 1) * P], looked_up(h), start=True, stop=True)
-                nodes = slice(h * PIECE_NODES, (h + 1) * PIECE_NODES)
-                nc.scalar.copy(whj[:, k, :, nodes], whj_ps[:].rearrange("p (n t) -> p t n", t=D))
+        def project(k, h, copy):
+            whj_ps = bank_psum.tile([P, PIECE], F32, name="whj_ps", tag="bank")
+            nc.tensor.matmul(whj_ps[:], w_sb[:, k * P : (k + 1) * P], looked_up(h), start=True, stop=True)
+            nodes = slice(h * PIECE_NODES, (h + 1) * PIECE_NODES)
+            copy(whj[:, k, :, nodes], whj_ps[:].rearrange("p (n t) -> p t n", t=D))
 
         def turn(k):
             slices = []
@@ -106,15 +105,11 @@ def tile_multihead_gaatn_kernel(tc, table, w, a1, a2, offs, out):
                 slices.append(bank)
             return slices
 
-        project(0)
+        project(0, 0, nc.scalar.copy)
+        project(0, 1, nc.scalar.copy)
         nb_t_ps = bank_psum.tile([P, D, SCORE_ROWS], F32, name="nb_t_ps", tag="bank")
         for t in range(D):
             nc.tensor.transpose(nb_t_ps[:, t, :], nb[:, t, :], identity[0:SCORE_ROWS, 0:SCORE_ROWS])
-        slices_of = []
-        for k in range(1, H):
-            project(k)
-            slices_of.append(turn(k - 1))
-        slices_of.append(turn(H - 1))
 
         by_node = [P, H, D]
         z_neg = held.tile(by_node, F32, name="z_neg")
@@ -134,28 +129,50 @@ def tile_multihead_gaatn_kernel(tc, table, w, a1, a2, offs, out):
             nc.scalar.activation(
                 p_exp[:, k, :], e_neg[:, k, :], ACT.Exp, bias=e_max_neg[:, k : k + 1], scale=-1.0, accum_out=p_sum[:, k : k + 1]
             )
+        project(1, 0, nc.scalar.copy)
+        project(1, 1, nc.vector.tensor_copy)
         p_inv = held.tile([P, H], F32, name="p_inv")
         nc.vector.reciprocal(p_inv[:], p_sum[:])
         att = held.tile(by_node, F32, name="att")
         nc.vector.tensor_tensor(att[:], p_exp[:], p_inv[:].unsqueeze(2).to_broadcast(by_node), ALU.mult)
 
-        half_bank = PER_BANK // 2
-        for k in range(H):
-            sums = [held.tile([P, P], F32, name="sum%d_%d" % (k, i)) for i in range(D // 2)]
-            for step in range(2):
-                for i in range(D // 2):
-                    t = (i // half_bank) * PER_BANK + PER_BANK - 1 - step * half_bank - i % half_bank
-                    piece = slices_of[k][t // PER_BANK][:, t % PER_BANK, :]
-                    weight = att[:, k, t : t + 1]
-                    if step == 0:
-                        nc.vector.tensor_scalar(sums[i][:], piece, weight, None, ALU.mult)
-                    else:
-                        nc.vector.scalar_tensor_tensor(sums[i][:], piece, weight, sums[i][:], ALU.mult, ALU.add)
+        slices_of = [turn(0)]
+        for k in range(2, H):
+            project(k, 0, nc.scalar.copy)
+            project(k, 1, nc.scalar.copy)
+            slices_of.append(turn(k - 1))
+
+        def weight(k, bank, t):
+            return att[:, k, bank * PER_BANK + t : bank * PER_BANK + t + 1]
+
+        def sum_neighbours(k):
+            banks_of_vector = range(D // PER_BANK) if k < H // 2 else range(1)
+            banks_of_scalar = range(len(banks_of_vector), D // PER_BANK)
+            pairs = [(bank, i) for bank in banks_of_vector for i in range(PER_BANK // 2)]
+            sums = [held.tile([P, P], F32, name="pair%d_%d_%d" % (k, bank, i)) for bank, i in pairs]
+            for (bank, i), part in zip(pairs, sums):
+                t = PER_BANK - 1 - i
+                nc.vector.tensor_scalar(part[:], slices_of[k][bank][:, t, :], weight(k, bank, t), None, ALU.mult)
+            for (bank, i), part in zip(pairs, sums):
+                t = PER_BANK // 2 - 1 - i
+                nc.vector.scalar_tensor_tensor(
+                    part[:], slices_of[k][bank][:, t, :], weight(k, bank, t), part[:], ALU.mult, ALU.add
+                )
+            for bank in banks_of_scalar:
+                for t in reversed(range(PER_BANK)):
+                    part = held.tile([P, P], F32, name="single%d_%d_%d" % (k, bank, t))
+                    nc.scalar.activation(part[:], slices_of[k][bank][:, t, :], ACT.Copy, scale=weight(k, bank, t))
+                    sums.append(part)
             result_ps = bank_psum.tile([P, PIECE], F32, name="result_ps", tag="bank")
-            for i in range(D // 2):
+            for i, part in enumerate(sums):
                 nc.tensor.matmul(
-                    result_ps[:, 0:P], sums[i][:], identity[:], start=(i == 0), stop=(i == D // 2 - 1), is_transpose=True
+                    result_ps[:, 0:P], part[:], identity[:], start=(i == 0), stop=(i == len(sums) - 1), is_transpose=True
                 )
             result = ring.tile([P, P], F32, name="result")
             nc.scalar.activation(result[:], result_ps[:, 0:P], ACT.Relu)
             nc.sync.dma_start(out[k * P : (k + 1) * P, :], result[:])
+
+        sum_neighbours(0)
+        slices_of.append(turn(H - 1))
+        for k in range(1, H):
+            sum_neighbours(k)

@@ -19,7 +19,10 @@ PIECE = 512
 N_PIECES = N // PIECE
 PIECE_NODES = PIECE // D
 PER_COL = 16
-SCORE_ROWS = 64
+GROUP = 32
+GROUPS = 4
+SCORE_ROWS = GROUPS * GROUP
+TURN = D // GROUPS
 PER_BANK = PIECE // P
 
 FLOPS = 2 * P * (H * P) * (N + P)
@@ -36,16 +39,14 @@ def tile_multihead_gaatn_kernel(tc, table, w, a1, a2, offs, out):
         nc.scalar.dma_start(w_sb[:], w)
         a2_all = held.tile([P, H * P], F32, name="a2_all")
         nc.sync.dma_start(a2_all[:], a2.rearrange("c o -> (c o)").partition_broadcast(P))
-        table_sb = held.tile([P, S], BF16, name="table_sb")
+        dest_sb = held.tile([P, P], BF16, name="dest_sb")
+        nc.scalar.dma_start(dest_sb[:], table[:, 0:P])
         offsets = held.tile([P, N // PER_COL], U16, name="offsets")
+        nc.sync.dma_start(offsets[:], offs)
+        table_sb = held.tile([P, S], BF16, name="table_sb")
+        nc.scalar.dma_start(table_sb[:], table)
         a1_all = held.tile([P, H * P], F32, name="a1_all")
-        chunk = S // 4
-        for c in range(4):
-            queue = nc.scalar if c % 2 == 0 else nc.sync
-            queue.dma_start(table_sb[:, c * chunk : (c + 1) * chunk], table[:, c * chunk : (c + 1) * chunk])
-            if c == 0:
-                nc.sync.dma_start(offsets[:], offs)
-        nc.sync.dma_start(a1_all[:], a1.rearrange("c o -> (c o)").partition_broadcast(P))
+        nc.scalar.dma_start(a1_all[:], a1.rearrange("c o -> (c o)").partition_broadcast(P))
 
         warm = held.tile([P, 1], F32, name="warm")
         nc.vector.memset(warm[:], 0.0)
@@ -65,36 +66,40 @@ def tile_multihead_gaatn_kernel(tc, table, w, a1, a2, offs, out):
 
         v = held.tile([P, H], F32, name="v")
         dot_with_row(v, w_sb, a2_all)
-        nc.vector.tensor_scalar_mul(v_weights[:, 0:H], v[:], -1.0)
+        nc.vector.tensor_scalar_mul(
+            v_weights[:].rearrange("p (g y) -> p g y", y=GROUP)[:, 0:GROUPS, 0:H],
+            v[:].unsqueeze(1).to_broadcast([P, GROUPS, H]),
+            -1.0,
+        )
 
         whd_ps = bank_psum.tile([P, H * P], F32, name="whd_ps", tag="bank")
-        nc.tensor.matmul(whd_ps[:], table_sb[:, 0:P], w_sb[:], start=True, stop=True)
+        nc.tensor.matmul(whd_ps[:], dest_sb[:], w_sb[:], start=True, stop=True)
         src = held.tile([P, H], F32, name="src")
         dot_with_row(src, whd_ps, a1_all)
 
-        piece_cols = PIECE // PER_COL
+        def looked_up(first, count):
+            return table_sb[:].indirect(offsets[:, first // PER_COL : (first + count) // PER_COL])
 
-        def looked_up(h):
-            return table_sb[:].indirect(offsets[:, h * piece_cols : (h + 1) * piece_cols])
-
-        nb = held.tile([SCORE_ROWS, D, P], F32, name="nb")
-        for h in range(N_PIECES):
+        nb = held.tile([SCORE_ROWS, TURN, P], F32, name="nb")
+        for h, copy in enumerate((nc.scalar.copy, nc.vector.tensor_copy)):
             nb_ps = bank_psum.tile([P, PIECE], F32, name="nb_ps", tag="bank")
-            nc.tensor.matmul(nb_ps[:], v_weights[:], looked_up(h), start=True, stop=True)
-            by_slice = nb_ps[0:SCORE_ROWS, :].rearrange("p (n t) -> p t n", t=D)
+            nc.tensor.matmul(nb_ps[:], v_weights[:], looked_up(h * PIECE, PIECE), start=True, stop=True)
+            by_slice = nb_ps[:].rearrange("p (n t) -> p t n", t=D)
             nodes = slice(h * PIECE_NODES, (h + 1) * PIECE_NODES)
-            if h % 2 == 0:
-                nc.scalar.copy(nb[:, :, nodes], by_slice)
-            else:
-                nc.vector.tensor_copy(nb[:, :, nodes], by_slice)
+            for g in range(GROUPS):
+                rows = slice(GROUP * g, GROUP * (g + 1))
+                copy(nb[rows, :, nodes], by_slice[rows, TURN * g : TURN * (g + 1), :])
 
         whj = held.tile([P, H, D, P], F32, name="whj")
 
-        def project(k, h, copy):
+        def project(k, first, count, copy):
             whj_ps = bank_psum.tile([P, PIECE], F32, name="whj_ps", tag="bank")
-            nc.tensor.matmul(whj_ps[:], w_sb[:, k * P : (k + 1) * P], looked_up(h), start=True, stop=True)
-            nodes = slice(h * PIECE_NODES, (h + 1) * PIECE_NODES)
-            copy(whj[:, k, :, nodes], whj_ps[:].rearrange("p (n t) -> p t n", t=D))
+            nc.tensor.matmul(
+                whj_ps[:, 0:count], w_sb[:, k * P : (k + 1) * P], looked_up(first, count), start=True, stop=True
+            )
+            copy(
+                whj[:, k, :, first // D : (first + count) // D], whj_ps[:, 0:count].rearrange("p (n t) -> p t n", t=D)
+            )
 
         def turn(k):
             slices = []
@@ -105,18 +110,22 @@ def tile_multihead_gaatn_kernel(tc, table, w, a1, a2, offs, out):
                 slices.append(bank)
             return slices
 
-        project(0, 0, nc.scalar.copy)
-        project(0, 1, nc.scalar.copy)
-        nb_t_ps = bank_psum.tile([P, D, SCORE_ROWS], F32, name="nb_t_ps", tag="bank")
-        for t in range(D):
-            nc.tensor.transpose(nb_t_ps[:, t, :], nb[:, t, :], identity[0:SCORE_ROWS, 0:SCORE_ROWS])
+        project(0, 0, PIECE, nc.scalar.copy)
+        project(0, PIECE, PIECE, nc.scalar.copy)
+        nb_t_bank = bank_psum.tile([P, PIECE], F32, name="nb_t_bank", tag="bank")
+        nb_t_ps = nb_t_bank[:, 0 : TURN * SCORE_ROWS].rearrange("p (t g y) -> p t g y", g=GROUPS, y=GROUP)
+        for t in range(TURN):
+            nc.tensor.transpose(
+                nb_t_bank[:, t * SCORE_ROWS : (t + 1) * SCORE_ROWS], nb[:, t, :], identity[0:SCORE_ROWS, 0:SCORE_ROWS]
+            )
 
         by_node = [P, H, D]
         z_neg = held.tile(by_node, F32, name="z_neg")
+        by_group = [P, H, GROUPS, TURN]
         nc.vector.tensor_tensor(
-            z_neg[:],
-            nb_t_ps[:, :, 0:H].rearrange("p t k -> p k t"),
-            src[:].unsqueeze(2).to_broadcast(by_node),
+            z_neg[:].rearrange("p k (g t) -> p k g t", g=GROUPS),
+            nb_t_ps[:, :, :, 0:H].rearrange("p t g k -> p k g t"),
+            src[:].unsqueeze(2).unsqueeze(2).to_broadcast(by_group),
             ALU.subtract,
         )
         e_neg = held.tile(by_node, F32, name="e_neg")
@@ -129,50 +138,74 @@ def tile_multihead_gaatn_kernel(tc, table, w, a1, a2, offs, out):
             nc.scalar.activation(
                 p_exp[:, k, :], e_neg[:, k, :], ACT.Exp, bias=e_max_neg[:, k : k + 1], scale=-1.0, accum_out=p_sum[:, k : k + 1]
             )
-        project(1, 0, nc.scalar.copy)
-        project(1, 1, nc.vector.tensor_copy)
+        project(1, 0, PIECE, nc.scalar.copy)
+        project(1, PIECE, PIECE, nc.vector.tensor_copy)
         p_inv = held.tile([P, H], F32, name="p_inv")
         nc.vector.reciprocal(p_inv[:], p_sum[:])
-        att = held.tile(by_node, F32, name="att")
-        nc.vector.tensor_tensor(att[:], p_exp[:], p_inv[:].unsqueeze(2).to_broadcast(by_node), ALU.mult)
 
-        slices_of = [turn(0)]
-        for k in range(2, H):
-            project(k, 0, nc.scalar.copy)
-            project(k, 1, nc.scalar.copy)
-            slices_of.append(turn(k - 1))
+        def weight(weights, k, bank, t):
+            return weights[:, k, bank * PER_BANK + t : bank * PER_BANK + t + 1]
 
-        def weight(k, bank, t):
-            return att[:, k, bank * PER_BANK + t : bank * PER_BANK + t + 1]
+        def first_of_pairs(k, banks, weights, inverse_sum=None):
+            parts = []
+            for bank in banks:
+                for i in range(PER_BANK // 2):
+                    t = PER_BANK - 1 - i
+                    part = held.tile([P, P], F32, name="pair%d_%d_%d" % (k, bank, i))
+                    piece = slices_of[k][bank][:, t, :]
+                    if inverse_sum is None:
+                        nc.vector.tensor_scalar(part[:], piece, weight(weights, k, bank, t), None, ALU.mult)
+                    else:
+                        nc.vector.tensor_scalar(
+                            part[:], piece, weight(weights, k, bank, t), inverse_sum, ALU.mult, ALU.mult
+                        )
+                    parts.append(part)
+            return parts
 
-        def sum_neighbours(k):
-            banks_of_vector = range(D // PER_BANK) if k < H // 2 else range(1)
-            banks_of_scalar = range(len(banks_of_vector), D // PER_BANK)
-            pairs = [(bank, i) for bank in banks_of_vector for i in range(PER_BANK // 2)]
-            sums = [held.tile([P, P], F32, name="pair%d_%d_%d" % (k, bank, i)) for bank, i in pairs]
-            for (bank, i), part in zip(pairs, sums):
-                t = PER_BANK - 1 - i
-                nc.vector.tensor_scalar(part[:], slices_of[k][bank][:, t, :], weight(k, bank, t), None, ALU.mult)
-            for (bank, i), part in zip(pairs, sums):
-                t = PER_BANK // 2 - 1 - i
-                nc.vector.scalar_tensor_tensor(
-                    part[:], slices_of[k][bank][:, t, :], weight(k, bank, t), part[:], ALU.mult, ALU.add
-                )
-            for bank in banks_of_scalar:
-                for t in reversed(range(PER_BANK)):
-                    part = held.tile([P, P], F32, name="single%d_%d_%d" % (k, bank, t))
-                    nc.scalar.activation(part[:], slices_of[k][bank][:, t, :], ACT.Copy, scale=weight(k, bank, t))
-                    sums.append(part)
+        def second_of_pairs(k, banks, weights, parts):
+            for bank in banks:
+                for i in range(PER_BANK // 2):
+                    t = PER_BANK // 2 - 1 - i
+                    part = parts[bank * (PER_BANK // 2) + i]
+                    nc.vector.scalar_tensor_tensor(
+                        part[:], slices_of[k][bank][:, t, :], weight(weights, k, bank, t), part[:], ALU.mult, ALU.add
+                    )
+
+        def turn_back(k, parts):
             result_ps = bank_psum.tile([P, PIECE], F32, name="result_ps", tag="bank")
-            for i, part in enumerate(sums):
+            for i, part in enumerate(parts):
                 nc.tensor.matmul(
-                    result_ps[:, 0:P], part[:], identity[:], start=(i == 0), stop=(i == len(sums) - 1), is_transpose=True
+                    result_ps[:, 0:P], part[:], identity[:], start=(i == 0), stop=(i == len(parts) - 1), is_transpose=True
                 )
             result = ring.tile([P, P], F32, name="result")
             nc.scalar.activation(result[:], result_ps[:, 0:P], ACT.Relu)
             nc.sync.dma_start(out[k * P : (k + 1) * P, :], result[:])
 
-        sum_neighbours(0)
-        slices_of.append(turn(H - 1))
+        both_banks = range(D // PER_BANK)
+        slices_of = [turn(0)]
+        sums_0 = first_of_pairs(0, both_banks, p_exp, p_inv[:, 0:1])
+        att = held.tile(by_node, F32, name="att")
+        nc.vector.tensor_tensor(att[:], p_exp[:], p_inv[:].unsqueeze(2).to_broadcast(by_node), ALU.mult)
+        second_of_pairs(0, both_banks, att, sums_0)
+        nc.gpsimd.tensor_tensor(sums_0[0][:], sums_0[0][:], sums_0[1][:], ALU.add)
+        nc.gpsimd.tensor_tensor(sums_0[2][:], sums_0[2][:], sums_0[3][:], ALU.add)
+        nc.gpsimd.tensor_tensor(sums_0[0][:], sums_0[0][:], sums_0[2][:], ALU.add)
+
+        for k in range(2, H):
+            project(k, 0, PIECE, nc.scalar.copy)
+            pieces = 1 if k < H - 1 else 2
+            for i in range(pieces):
+                project(k, PIECE + i * (PIECE // pieces), PIECE // pieces, nc.scalar.copy)
+
         for k in range(1, H):
-            sum_neighbours(k)
+            slices_of.append(turn(k))
+        for k in range(1, H):
+            sums = first_of_pairs(k, [0], att)
+            second_of_pairs(k, [0], att, sums)
+            for t in reversed(range(PER_BANK)):
+                part = held.tile([P, P], F32, name="single%d_%d" % (k, t))
+                nc.scalar.activation(part[:], slices_of[k][1][:, t, :], ACT.Copy, scale=weight(att, k, 1, t))
+                sums.append(part)
+            turn_back(k, sums)
+            if k == 1:
+                turn_back(0, sums_0[0:1])

import concourse.mybir as mybir
from concourse.masks import make_identity

F32 = mybir.dt.float32
BF16 = mybir.dt.bfloat16
U16 = mybir.dt.uint16
ALU = mybir.AluOpType
ACT = mybir.ActivationFunctionType
X = mybir.AxisListType.X

P = 128
S = 2048
H = 4
D = 8
N = P * D
SLOPE = 0.01

PIECE = 512
N_PIECES = N // PIECE
PIECE_NODES = PIECE // D
PER_COL = 16
GROUP = 32
GROUPS = 4
SCORE_ROWS = GROUPS * GROUP
TURN = D // GROUPS
PER_BANK = PIECE // P

FLOPS = 2 * P * (H * P) * (N + P)


def tile_multihead_gaatn_kernel(tc, table, w, a1, a2, offs, out):
    nc = tc.nc
    with (
        tc.tile_pool(name="held", bufs=1) as held,
        tc.tile_pool(name="ring", bufs=4) as ring,
        tc.psum_pool(name="bank_psum", bufs=8) as bank_psum,
    ):
        w_sb = held.tile([P, H * P], BF16, name="w_sb")
        nc.scalar.dma_start(w_sb[:], w)
        a2_all = held.tile([P, H * P], F32, name="a2_all")
        nc.sync.dma_start(a2_all[:], a2.rearrange("c o -> (c o)").partition_broadcast(P))
        dest_sb = held.tile([P, P], BF16, name="dest_sb")
        nc.scalar.dma_start(dest_sb[:], table[:, 0:P])
        offsets = held.tile([P, N // PER_COL], U16, name="offsets")
        nc.sync.dma_start(offsets[:], offs)
        table_sb = held.tile([P, S], BF16, name="table_sb")
        nc.scalar.dma_start(table_sb[:], table)
        a1_all = held.tile([P, H * P], F32, name="a1_all")
        nc.scalar.dma_start(a1_all[:], a1.rearrange("c o -> (c o)").partition_broadcast(P))

        warm = held.tile([P, 1], F32, name="warm")
        nc.vector.memset(warm[:], 0.0)
        nc.scalar.activation(warm[:], warm[:], ACT.Exp)
        v_weights = held.tile([P, P], BF16, name="v_weights")
        nc.gpsimd.memset(v_weights[:], 0.0)
        identity = held.tile([P, P], F32, name="identity")
        make_identity(nc, identity[:])

        def dot_with_row(sums, rows, row):
            for k in range(H):
                head = slice(k * P, (k + 1) * P)
                products = ring.tile([P, P], F32, name="products")
                nc.vector.scalar_tensor_tensor(
                    products[:], rows[:, head], 1.0, row[:, head], ALU.mult, ALU.mult, accum_out=sums[:, k : k + 1]
                )

        v = held.tile([P, H], F32, name="v")
        dot_with_row(v, w_sb, a2_all)
        nc.vector.tensor_scalar_mul(
            v_weights[:].rearrange("p (g y) -> p g y", y=GROUP)[:, 0:GROUPS, 0:H],
            v[:].unsqueeze(1).to_broadcast([P, GROUPS, H]),
            -1.0,
        )

        whd_ps = bank_psum.tile([P, H * P], F32, name="whd_ps", tag="bank")
        nc.tensor.matmul(whd_ps[:], dest_sb[:], w_sb[:], start=True, stop=True)
        src = held.tile([P, H], F32, name="src")
        dot_with_row(src, whd_ps, a1_all)

        def looked_up(first, count):
            return table_sb[:].indirect(offsets[:, first // PER_COL : (first + count) // PER_COL])

        nb = held.tile([SCORE_ROWS, TURN, P], F32, name="nb")
        for h, copy in enumerate((nc.scalar.copy, nc.vector.tensor_copy)):
            nb_ps = bank_psum.tile([P, PIECE], F32, name="nb_ps", tag="bank")
            nc.tensor.matmul(nb_ps[:], v_weights[:], looked_up(h * PIECE, PIECE), start=True, stop=True)
            by_slice = nb_ps[:].rearrange("p (n t) -> p t n", t=D)
            nodes = slice(h * PIECE_NODES, (h + 1) * PIECE_NODES)
            for g in range(GROUPS):
                rows = slice(GROUP * g, GROUP * (g + 1))
                copy(nb[rows, :, nodes], by_slice[rows, TURN * g : TURN * (g + 1), :])

        whj = held.tile([P, H, D, P], F32, name="whj")

        def project(k, first, count, copy):
            whj_ps = bank_psum.tile([P, PIECE], F32, name="whj_ps", tag="bank")
            nc.tensor.matmul(
                whj_ps[:, 0:count], w_sb[:, k * P : (k + 1) * P], looked_up(first, count), start=True, stop=True
            )
            copy(
                whj[:, k, :, first // D : (first + count) // D], whj_ps[:, 0:count].rearrange("p (n t) -> p t n", t=D)
            )

        def turn(k):
            slices = []
            for first in range(0, D, PER_BANK):
                bank = bank_psum.tile([P, PER_BANK, P], F32, name="slices_ps", tag="bank")
                for t in range(first, first + PER_BANK):
                    nc.tensor.transpose(bank[:, t - first, :], whj[:, k, t, :], identity[:])
                slices.append(bank)
            return slices

        project(0, 0, PIECE, nc.scalar.copy)
        project(0, PIECE, PIECE, nc.scalar.copy)
        nb_t_bank = bank_psum.tile([P, PIECE], F32, name="nb_t_bank", tag="bank")
        nb_t_ps = nb_t_bank[:, 0 : TURN * SCORE_ROWS].rearrange("p (t g y) -> p t g y", g=GROUPS, y=GROUP)
        for t in range(TURN):
            nc.tensor.transpose(
                nb_t_bank[:, t * SCORE_ROWS : (t + 1) * SCORE_ROWS], nb[:, t, :], identity[0:SCORE_ROWS, 0:SCORE_ROWS]
            )

        by_node = [P, H, D]
        z_neg = held.tile(by_node, F32, name="z_neg")
        by_group = [P, H, GROUPS, TURN]
        nc.vector.tensor_tensor(
            z_neg[:].rearrange("p k (g t) -> p k g t", g=GROUPS),
            nb_t_ps[:, :, :, 0:H].rearrange("p t g k -> p k g t"),
            src[:].unsqueeze(2).unsqueeze(2).to_broadcast(by_group),
            ALU.subtract,
        )
        e_neg = held.tile(by_node, F32, name="e_neg")
        nc.vector.scalar_tensor_tensor(e_neg[:], z_neg[:], SLOPE, z_neg[:], ALU.mult, ALU.min)
        e_max_neg = held.tile([P, H], F32, name="e_max_neg")
        nc.vector.tensor_reduce(e_max_neg[:], e_neg[:], X, ALU.min)
        p_exp = held.tile(by_node, F32, name="p_exp")
        p_sum = held.tile([P, H], F32, name="p_sum")
        for k in range(H):
            nc.scalar.activation(
                p_exp[:, k, :], e_neg[:, k, :], ACT.Exp, bias=e_max_neg[:, k : k + 1], scale=-1.0, accum_out=p_sum[:, k : k + 1]
            )
        project(1, 0, PIECE, nc.scalar.copy)
        project(1, PIECE, PIECE, nc.vector.tensor_copy)
        p_inv = held.tile([P, H], F32, name="p_inv")
        nc.vector.reciprocal(p_inv[:], p_sum[:])

        def weight(weights, k, bank, t):
            return weights[:, k, bank * PER_BANK + t : bank * PER_BANK + t + 1]

        def first_of_pairs(k, banks, weights, inverse_sum=None):
            parts = []
            for bank in banks:
                for i in range(PER_BANK // 2):
                    t = PER_BANK - 1 - i
                    part = held.tile([P, P], F32, name="pair%d_%d_%d" % (k, bank, i))
                    piece = slices_of[k][bank][:, t, :]
                    if inverse_sum is None:
                        nc.vector.tensor_scalar(part[:], piece, weight(weights, k, bank, t), None, ALU.mult)
                    else:
                        nc.vector.tensor_scalar(
                            part[:], piece, weight(weights, k, bank, t), inverse_sum, ALU.mult, ALU.mult
                        )
                    parts.append(part)
            return parts

        def second_of_pairs(k, banks, weights, parts):
            for bank in banks:
                for i in range(PER_BANK // 2):
                    t = PER_BANK // 2 - 1 - i
                    part = parts[bank * (PER_BANK // 2) + i]
                    nc.vector.scalar_tensor_tensor(
                        part[:], slices_of[k][bank][:, t, :], weight(weights, k, bank, t), part[:], ALU.mult, ALU.add
                    )

        def turn_back(k, parts):
            result_ps = bank_psum.tile([P, PIECE], F32, name="result_ps", tag="bank")
            for i, part in enumerate(parts):
                nc.tensor.matmul(
                    result_ps[:, 0:P], part[:], identity[:], start=(i == 0), stop=(i == len(parts) - 1), is_transpose=True
                )
            result = ring.tile([P, P], F32, name="result")
            nc.scalar.activation(result[:], result_ps[:, 0:P], ACT.Relu)
            nc.sync.dma_start(out[k * P : (k + 1) * P, :], result[:])

        both_banks = range(D // PER_BANK)
        slices_of = [turn(0)]
        sums_0 = first_of_pairs(0, both_banks, p_exp, p_inv[:, 0:1])
        att = held.tile(by_node, F32, name="att")
        nc.vector.tensor_tensor(att[:], p_exp[:], p_inv[:].unsqueeze(2).to_broadcast(by_node), ALU.mult)
        second_of_pairs(0, both_banks, att, sums_0)
        nc.gpsimd.tensor_tensor(sums_0[0][:], sums_0[0][:], sums_0[1][:], ALU.add)
        nc.gpsimd.tensor_tensor(sums_0[2][:], sums_0[2][:], sums_0[3][:], ALU.add)
        nc.gpsimd.tensor_tensor(sums_0[0][:], sums_0[0][:], sums_0[2][:], ALU.add)

        for k in range(2, H):
            project(k, 0, PIECE, nc.scalar.copy)
            pieces = 1 if k < H - 1 else 2
            for i in range(pieces):
                project(k, PIECE + i * (PIECE // pieces), PIECE // pieces, nc.scalar.copy)

        for k in range(1, H):
            slices_of.append(turn(k))
        for k in range(1, H):
            sums = first_of_pairs(k, [0], att)
            second_of_pairs(k, [0], att, sums)
            for t in reversed(range(PER_BANK)):
                part = held.tile([P, P], F32, name="single%d_%d" % (k, t))
                nc.scalar.activation(part[:], slices_of[k][1][:, t, :], ACT.Copy, scale=weight(att, k, 1, t))
                sums.append(part)
            turn_back(k, sums)
            if k == 1:
                turn_back(0, sums_0[0:1])
